import numpy as np
import ml_dtypes


def mxq(x, axis, fmt="e4m3"):
    dtype, down = {"e4m3": (ml_dtypes.float8_e4m3fn, 7), "e5m2": (ml_dtypes.float8_e5m2, 14)}[fmt]
    v = np.moveaxis(np.asarray(x, np.float32).astype(ml_dtypes.bfloat16).astype(np.float64), axis, -1)
    blocks = v.reshape(v.shape[:-1] + (-1, 32))
    amax = np.abs(blocks).max(-1, keepdims=True)
    byte = np.maximum(np.where(amax > 0, np.frexp(amax)[1] - 1 + 127, 0) - down, 1)
    scale = np.exp2(byte - 127.0)
    codes = (blocks / scale).astype(np.float32).astype(dtype).astype(np.float64)
    return np.moveaxis((codes * scale).reshape(v.shape), -1, axis)


WIDE = False


def mx_kscale(k):
    if not WIDE:
        return np.ones(k)
    levels = np.array([20, -20, 10, -10, 0])
    a = np.random.permutation(np.resize(levels, k // 512 * 4)).reshape(k // 512, 4)
    idx = np.arange(k)
    return np.exp2(a[idx // 512, idx % 128 // 32])


BF16 = ml_dtypes.bfloat16


def bf(x):
    return np.asarray(x, np.float32).astype(BF16)


def f64(x):
    return np.asarray(x).astype(np.float64)


B, CIN, COUT, T, F, KH, KW, PH, PW = 2, 256, 512, 256, 8, 3, 3, 1, 1
OT = T + PH + PH - KH + 1


def setup_inputs():
    u = mx_kscale(COUT)
    x = np.random.standard_normal((B, CIN, T, F))
    kernel = np.random.standard_normal((COUT, CIN, F, KH, KW)) / np.sqrt(CIN * KH * KW) / u[:, None, None, None, None]
    bias = np.random.standard_normal((1, COUT, 1, F)) * 0.5
    g = np.random.standard_normal((B, COUT, OT, F)) * np.exp2(np.random.randint(-12, 1, (B, 1, OT, F))) * 16.0 * u[None, :, None, None]
    return {"x": bf(x), "kernel": bf(kernel), "bias": bf(bias), "grad_out": bf(g)}


def reference(x, kernel, bias, grad_out):
    gq = mxq(f64(grad_out).transpose(3, 2, 0, 1).reshape(F, OT * B, COUT), 2, "e5m2")
    kt = f64(kernel).transpose(2, 3, 4, 0, 1)
    gx = np.zeros((F, T * B, CIN))
    for m in range(KH):
        for n in range(KW):
            f0, f1 = max(0, PW - n), min(F, F + PW - n)
            t0, t1 = max(0, PH - m), min(OT, T + PH - m)
            p = gq[f0:f1] @ mxq(kt[f0:f1, m, n], 1, "e4m3")
            gx[f0 + n - PW:f1 + n - PW, (t0 + m - PH) * B:(t1 + m - PH) * B] += p[:, t0 * B:t1 * B]
    return np.ascontiguousarray(gx.reshape(F, T, B, CIN).transpose(2, 3, 1, 0))

@@ -1,0 +1,184 @@
+from contextlib import ExitStack
+
+import concourse.mybir as mybir
+
+BF16 = mybir.dt.bfloat16
+F32 = mybir.dt.float32
+U32 = mybir.dt.uint32
+U8 = mybir.dt.uint8
+E4M3_X4 = mybir.dt.float8_e4m3fn_x4
+E5M2_X4 = mybir.dt.float8_e5m2_x4
+
+P = 128
+PACK = 4
+BATCH, CIN, COUT, FRAMES, BINS, KH, KW, PH, PW = 2, 256, 512, 256, 8, 3, 3, 1, 1
+assert COUT == P * PACK
+
+TAPS = KH * KW
+ROW = BINS * TAPS
+N_COLS = BATCH * FRAMES
+
+PHASES = 8
+STEPS = FRAMES // PHASES
+PLANE = BATCH * STEPS
+PLANES = PHASES + 2 * PH
+G_COLS = PLANES * PLANE
+
+CHUNK = 32
+CHUNKS_PER_TILE = P // CHUNK
+I_TILES = CIN // P
+RAW_BUFS = 3
+WIDEST_QUANTISE = 4096
+HALF_BINS = BINS // 2
+
+FLOPS = 2 * COUT * N_COLS * CIN * (BINS * TAPS - 2 * KH)
+BYTES = 2 * COUT * CIN * (BINS * TAPS - 2 * KH) + 2 * BATCH * COUT * FRAMES * BINS + 4 * BATCH * CIN * FRAMES * BINS
+
+
+def kept_n(f):
+    return [n for n in range(KW) if 0 <= f + n - PW < BINS]
+
+
+def slot(f, m, n):
+    kept = kept_n(f)
+    if len(kept) == KW:
+        return m * KW + n
+    return kept.index(n) * KH + m
+
+
+def power_of_two_pieces(width):
+    pieces = []
+    start = 0
+    size = WIDEST_QUANTISE
+    while start < width:
+        if start + size <= width:
+            pieces.append((start, size))
+            start += size
+        else:
+            size //= 2
+    return pieces
+
+
+def tile_svconv2d_pa_kernel(tc, x, kernel, bias, grad_out, out):
+    nc = tc.nc
+
+    def copy_engine(f):
+        if f % 2 == 1 and f < BINS - 1:
+            return nc.scalar.copy
+        return nc.vector.tensor_copy
+
+    with ExitStack() as ctx:
+        g_pool = ctx.enter_context(tc.tile_pool(name="g_quantised", bufs=1))
+        raw_pool = ctx.enter_context(tc.tile_pool(name="raw", bufs=RAW_BUFS))
+        grouped_pool = ctx.enter_context(tc.tile_pool(name="grouped", bufs=1))
+        psum = ctx.enter_context(tc.psum_pool(name="psum", bufs=8))
+
+        kernel_rows = kernel.rearrange("(p j) i f m n -> p j (i f m n)", j=PACK)
+
+        def load_chunk(c):
+            raw = raw_pool.tile([P, PACK, CHUNK * ROW], BF16, name="raw")
+            nc.sync.dma_start(out=raw[:], in_=kernel_rows[:, :, c * CHUNK * ROW : (c + 1) * CHUNK * ROW])
+            return raw
+
+        g_codes = g_pool.tile([P, BINS * G_COLS], U32, align_bytes=64)
+        g_scales = g_pool.tile([P, BINS * G_COLS], U8, align_bytes=64)
+
+        raws = []
+        with tc.tile_pool(name="g_prepare", bufs=1) as g_prepare:
+            g_raw = g_prepare.tile([P, BATCH, PACK, FRAMES * BINS], BF16)
+            for b in range(BATCH):
+                nc.sync.dma_start(out=g_raw[:, b], in_=grad_out[b].rearrange("(p j) t f -> p j (t f)", j=PACK))
+            for c in range(RAW_BUFS):
+                raws.append(load_chunk(c))
+
+            g_grouped = g_prepare.tile([P, BINS, PLANES, BATCH, STEPS, PACK], BF16, align_bytes=64)
+            nc.vector.memset(g_grouped[:, :, 0, :, 0, :], 0.0)
+            nc.vector.memset(g_grouped[:, :, PLANES - 1, :, STEPS - 1, :], 0.0)
+            for f in range(BINS):
+                for b in range(BATCH):
+                    by_bin = g_raw[:, b].rearrange("p j (q r f) -> p f r q j", r=PHASES, f=BINS)
+                    copy_engine(f)(out=g_grouped[:, f, PH : PH + PHASES, b], in_=by_bin[:, f])
+            nc.vector.tensor_copy(
+                out=g_grouped[:, :, 0, :, 1:STEPS, :], in_=g_grouped[:, :, PHASES, :, 0 : STEPS - 1, :]
+            )
+            nc.vector.tensor_copy(
+                out=g_grouped[:, :, PLANES - 1, :, 0 : STEPS - 1, :], in_=g_grouped[:, :, PH, :, 1:STEPS, :]
+            )
+            g_flat = g_grouped[:].rearrange("p f s b q j -> p (f s b q j)")
+            for start, size in power_of_two_pieces(BINS * G_COLS * PACK):
+                words = slice(start // PACK, (start + size) // PACK)
+                nc.vector.quantize_mx(
+                    out=g_codes[:, words].bitcast(E5M2_X4),
+                    scales=g_scales[:, words],
+                    in_=g_flat[:, start : start + size],
+                )
+
+        late = ctx.enter_context(tc.tile_pool(name="late", bufs=1))
+
+        for it in range(I_TILES):
+            grouped = [
+                grouped_pool.tile([P, len(kept_n(f)) * KH, P, PACK], BF16, name="grouped%d" % f, align_bytes=64)
+                for f in range(BINS)
+            ]
+            for cl in range(CHUNKS_PER_TILE):
+                c = it * CHUNKS_PER_TILE + cl
+                taps_first = raws[c][:].rearrange("p j (i w) -> p w i j", w=ROW)
+                cols = slice(cl * CHUNK, (cl + 1) * CHUNK)
+                for f in range(BINS):
+                    kept = kept_n(f)
+                    if len(kept) == KW:
+                        copy_engine(f)(out=grouped[f][:, :, cols, :], in_=taps_first[:, f * TAPS : (f + 1) * TAPS])
+                    else:
+                        for s, n in enumerate(kept):
+                            copy_engine(f)(
+                                out=grouped[f][:, s * KH : (s + 1) * KH, cols, :],
+                                in_=taps_first[:, f * TAPS + n : (f + 1) * TAPS : KW],
+                            )
+                if c + RAW_BUFS < I_TILES * CHUNKS_PER_TILE:
+                    raws.append(load_chunk(c + RAW_BUFS))
+
+            codes = []
+            scales = []
+            for f in range(BINS):
+                width = len(kept_n(f)) * KH * P
+                codes.append(late.tile([P, width], U32, name="codes%d" % f, align_bytes=64))
+                scales.append(late.tile([P, width], U8, name="scales%d" % f, align_bytes=64))
+                flat = grouped[f][:].rearrange("p s i j -> p (s i j)")
+                for start, size in power_of_two_pieces(width * PACK):
+                    words = slice(start // PACK, (start + size) // PACK)
+                    nc.vector.quantize_mx(
+                        out=codes[f][:, words].bitcast(E4M3_X4),
+                        scales=scales[f][:, words],
+                        in_=flat[:, start : start + size],
+                    )
+
+            planes = late.tile([P, BINS, N_COLS], F32, name="planes")
+            result = late.tile([P, N_COLS, BINS], F32, name="result")
+            for fo in range(BINS):
+                acc = psum.tile([P, N_COLS], F32, name="acc")
+                terms = [(fo + PW - n, m, n) for n in reversed(range(KW)) for m in range(KH) if 0 <= fo + PW - n < BINS]
+                for k, (f, m, n) in enumerate(terms):
+                    w_cols = slice(slot(f, m, n) * P, (slot(f, m, n) + 1) * P)
+                    first = f * G_COLS + (PH + PH - m) * PLANE
+                    g_cols = slice(first, first + N_COLS)
+                    nc.tensor.matmul_mx(
+                        out=acc[:],
+                        lhsT=codes[f][:, w_cols].bitcast(E4M3_X4),
+                        lhsT_scale=scales[f][:, w_cols],
+                        rhs=g_codes[:, g_cols].bitcast(E5M2_X4),
+                        rhs_scale=g_scales[:, g_cols],
+                        start=(k == 0),
+                        stop=(k == len(terms) - 1),
+                    )
+                nc.scalar.copy(
+                    out=planes[:, fo].rearrange("p (b q r) -> p b q r", b=BATCH, q=STEPS),
+                    in_=acc[:].rearrange("p (r b q) -> p b q r", r=PHASES, b=BATCH),
+                )
+                if fo % HALF_BINS == HALF_BINS - 1:
+                    half = slice(fo + 1 - HALF_BINS, fo + 1)
+                    nc.vector.tensor_copy(out=result[:, :, half], in_=planes[:, half, :].rearrange("p f c -> p c f"))
+            for b in range(BATCH):
+                nc.sync.dma_start(
+                    out=out[b, it * P : (it + 1) * P].rearrange("i t f -> i (t f)"),
+                    in_=result[:, b * FRAMES : (b + 1) * FRAMES, :].rearrange("p t f -> p (t f)"),
+                )

@@ -41,9 +41,7 @@ def kept_n(f):
 
 def slot(f, m, n):
     kept = kept_n(f)
-    if len(kept) == KW:
-        return m * KW + n
-    return kept.index(n) * KH + m
+    return m * len(kept) + kept.index(n)
 
 
 def power_of_two_pieces(width):
@@ -62,10 +60,12 @@ def power_of_two_pieces(width):
 def tile_svconv2d_pa_kernel(tc, x, kernel, bias, grad_out, out):
     nc = tc.nc
 
-    def copy_engine(f):
-        if f % 2 == 1 and f < BINS - 1:
-            return nc.scalar.copy
-        return nc.vector.tensor_copy
+    def regroup(on_scalar, dst, src):
+        if on_scalar:
+            for a in range(dst.shape[1]):
+                nc.scalar.copy(out=dst[:, a], in_=src[:, a])
+        else:
+            nc.vector.tensor_copy(out=dst, in_=src)
 
     with ExitStack() as ctx:
         g_pool = ctx.enter_context(tc.tile_pool(name="g_quantised", bufs=1))
@@ -94,10 +94,12 @@ def tile_svconv2d_pa_kernel(tc, x, kernel, bias, grad_out, out):
             g_grouped = g_prepare.tile([P, BINS, PLANES, BATCH, STEPS, PACK], BF16, align_bytes=64)
             nc.vector.memset(g_grouped[:, :, 0, :, 0, :], 0.0)
             nc.vector.memset(g_grouped[:, :, PLANES - 1, :, STEPS - 1, :], 0.0)
-            for f in range(BINS):
-                for b in range(BATCH):
-                    by_bin = g_raw[:, b].rearrange("p j (q r f) -> p f r q j", r=PHASES, f=BINS)
-                    copy_engine(f)(out=g_grouped[:, f, PH : PH + PHASES, b], in_=by_bin[:, f])
+            for b in range(BATCH):
+                g_src = g_raw[:, b].rearrange("p j (q r f) -> p r q j f", r=PHASES, f=BINS)
+                g_dst = g_grouped[:, :, PH : PH + PHASES, b].rearrange("p f r q j -> p r q j f")
+                for h in range(BINS // HALF_BINS):
+                    half = slice(h * HALF_BINS, (h + 1) * HALF_BINS)
+                    regroup(b == 1, g_dst[:, :, :, :, half], g_src[:, :, :, :, half])
             nc.vector.tensor_copy(
                 out=g_grouped[:, :, 0, :, 1:STEPS, :], in_=g_grouped[:, :, PHASES, :, 0 : STEPS - 1, :]
             )
@@ -122,18 +124,12 @@ def tile_svconv2d_pa_kernel(tc, x, kernel, bias, grad_out, out):
             ]
             for cl in range(CHUNKS_PER_TILE):
                 c = it * CHUNKS_PER_TILE + cl
-                taps_first = raws[c][:].rearrange("p j (i w) -> p w i j", w=ROW)
+                w_src = raws[c][:].rearrange("p j (i f m n) -> p f m i j n", f=BINS, m=KH, n=KW)
                 cols = slice(cl * CHUNK, (cl + 1) * CHUNK)
                 for f in range(BINS):
                     kept = kept_n(f)
-                    if len(kept) == KW:
-                        copy_engine(f)(out=grouped[f][:, :, cols, :], in_=taps_first[:, f * TAPS : (f + 1) * TAPS])
-                    else:
-                        for s, n in enumerate(kept):
-                            copy_engine(f)(
-                                out=grouped[f][:, s * KH : (s + 1) * KH, cols, :],
-                                in_=taps_first[:, f * TAPS + n : (f + 1) * TAPS : KW],
-                            )
+                    w_dst = grouped[f][:, :, cols, :].rearrange("p (m n) i j -> p m i j n", m=KH)
+                    regroup(f % 2 == 1 and f < BINS - 1, w_dst, w_src[:, f, :, :, :, kept[0] : kept[-1] + 1])
                 if c + RAW_BUFS < I_TILES * CHUNKS_PER_TILE:
                     raws.append(load_chunk(c + RAW_BUFS))
 

@@ -27,9 +27,12 @@ G_COLS = PLANES * PLANE
 CHUNK = 32
 CHUNKS_PER_TILE = P // CHUNK
 I_TILES = CIN // P
+N_CHUNKS = I_TILES * CHUNKS_PER_TILE
 RAW_BUFS = 3
 WIDEST_QUANTISE = 4096
 HALF_BINS = BINS // 2
+HALVES = 2
+BINS_PER_PART = BINS // CHUNKS_PER_TILE
 
 FLOPS = 2 * COUT * N_COLS * CIN * (BINS * TAPS - 2 * KH)
 BYTES = 2 * COUT * CIN * (BINS * TAPS - 2 * KH) + 2 * BATCH * COUT * FRAMES * BINS + 4 * BATCH * CIN * FRAMES * BINS
@@ -67,29 +70,37 @@ def tile_svconv2d_pa_kernel(tc, x, kernel, bias, grad_out, out):
         else:
             nc.vector.tensor_copy(out=dst, in_=src)
 
+    def quantise(x4, codes, scales, grouped_flat):
+        for start, size in power_of_two_pieces(grouped_flat.shape[1]):
+            words = slice(start // PACK, (start + size) // PACK)
+            nc.vector.quantize_mx(
+                out=codes[:, words].bitcast(x4), scales=scales[:, words], in_=grouped_flat[:, start : start + size]
+            )
+
     with ExitStack() as ctx:
+        ctx.enter_context(tc.manual_schedule())
         g_pool = ctx.enter_context(tc.tile_pool(name="g_quantised", bufs=1))
         raw_pool = ctx.enter_context(tc.tile_pool(name="raw", bufs=RAW_BUFS))
         grouped_pool = ctx.enter_context(tc.tile_pool(name="grouped", bufs=1))
-        psum = ctx.enter_context(tc.psum_pool(name="psum", bufs=8))
+        psum = ctx.enter_context(tc.psum_pool(name="psum", bufs=BINS))
 
         kernel_rows = kernel.rearrange("(p j) i f m n -> p j (i f m n)", j=PACK)
+        raws = []
 
         def load_chunk(c):
-            raw = raw_pool.tile([P, PACK, CHUNK * ROW], BF16, name="raw")
-            nc.sync.dma_start(out=raw[:], in_=kernel_rows[:, :, c * CHUNK * ROW : (c + 1) * CHUNK * ROW])
-            return raw
+            if c < N_CHUNKS:
+                raw = raw_pool.tile([P, PACK, CHUNK * ROW], BF16, name="raw")
+                nc.sync.dma_start(out=raw[:], in_=kernel_rows[:, :, c * CHUNK * ROW : (c + 1) * CHUNK * ROW])
+                raws.append(raw)
 
         g_codes = g_pool.tile([P, BINS * G_COLS], U32, align_bytes=64)
         g_scales = g_pool.tile([P, BINS * G_COLS], U8, align_bytes=64)
-
-        raws = []
         with tc.tile_pool(name="g_prepare", bufs=1) as g_prepare:
             g_raw = g_prepare.tile([P, BATCH, PACK, FRAMES * BINS], BF16)
             for b in range(BATCH):
                 nc.sync.dma_start(out=g_raw[:, b], in_=grad_out[b].rearrange("(p j) t f -> p j (t f)", j=PACK))
             for c in range(RAW_BUFS):
-                raws.append(load_chunk(c))
+                load_chunk(c)
 
             g_grouped = g_prepare.tile([P, BINS, PLANES, BATCH, STEPS, PACK], BF16, align_bytes=64)
             nc.vector.memset(g_grouped[:, :, 0, :, 0, :], 0.0)
@@ -97,84 +108,98 @@ def tile_svconv2d_pa_kernel(tc, x, kernel, bias, grad_out, out):
             for b in range(BATCH):
                 g_src = g_raw[:, b].rearrange("p j (q r f) -> p r q j f", r=PHASES, f=BINS)
                 g_dst = g_grouped[:, :, PH : PH + PHASES, b].rearrange("p f r q j -> p r q j f")
-                for h in range(BINS // HALF_BINS):
+                for h in range(HALVES):
                     half = slice(h * HALF_BINS, (h + 1) * HALF_BINS)
-                    regroup(b == 1, g_dst[:, :, :, :, half], g_src[:, :, :, :, half])
-            nc.vector.tensor_copy(
-                out=g_grouped[:, :, 0, :, 1:STEPS, :], in_=g_grouped[:, :, PHASES, :, 0 : STEPS - 1, :]
-            )
-            nc.vector.tensor_copy(
-                out=g_grouped[:, :, PLANES - 1, :, 0 : STEPS - 1, :], in_=g_grouped[:, :, PH, :, 1:STEPS, :]
-            )
-            g_flat = g_grouped[:].rearrange("p f s b q j -> p (f s b q j)")
-            for start, size in power_of_two_pieces(BINS * G_COLS * PACK):
-                words = slice(start // PACK, (start + size) // PACK)
-                nc.vector.quantize_mx(
-                    out=g_codes[:, words].bitcast(E5M2_X4),
-                    scales=g_scales[:, words],
-                    in_=g_flat[:, start : start + size],
+                    regroup(h == 1, g_dst[:, :, :, :, half], g_src[:, :, :, :, half])
+            for h in range(HALVES):
+                half = slice(h * HALF_BINS, (h + 1) * HALF_BINS)
+                nc.vector.tensor_copy(
+                    out=g_grouped[:, half, 0, :, 1:STEPS, :], in_=g_grouped[:, half, PHASES, :, 0 : STEPS - 1, :]
+                )
+                nc.vector.tensor_copy(
+                    out=g_grouped[:, half, PLANES - 1, :, 0 : STEPS - 1, :], in_=g_grouped[:, half, PH, :, 1:STEPS, :]
+                )
+                words = slice(h * HALF_BINS * G_COLS, (h + 1) * HALF_BINS * G_COLS)
+                quantise(
+                    E5M2_X4,
+                    g_codes[:, words],
+                    g_scales[:, words],
+                    g_grouped[:, half].rearrange("p f s b q j -> p (f s b q j)"),
                 )
 
         late = ctx.enter_context(tc.tile_pool(name="late", bufs=1))
+        finish_pool = ctx.enter_context(tc.tile_pool(name="finish", bufs=2))
 
+        def regroup_kernel(c, f, grouped):
+            kept = kept_n(f)
+            cols = slice((c % CHUNKS_PER_TILE) * CHUNK, (c % CHUNKS_PER_TILE + 1) * CHUNK)
+            w_src = raws[c][:].rearrange("p j (i f m n) -> p f m i j n", f=BINS, m=KH, n=KW)
+            w_dst = grouped[f][:, :, cols, :].rearrange("p (m n) i j -> p m i j n", m=KH)
+            regroup(f % 2 == 1 and f < BINS - 1, w_dst, w_src[:, f, :, :, :, kept[0] : kept[-1] + 1])
+
+        def multiply(fo, codes, scales):
+            acc = psum.tile([P, N_COLS], F32, name="acc")
+            terms = [(fo + PW - n, m, n) for n in reversed(range(KW)) for m in range(KH) if 0 <= fo + PW - n < BINS]
+            for k, (f, m, n) in enumerate(terms):
+                w_cols = slice(slot(f, m, n) * P, (slot(f, m, n) + 1) * P)
+                first = f * G_COLS + (PH + PH - m) * PLANE
+                g_cols = slice(first, first + N_COLS)
+                nc.tensor.matmul_mx(
+                    out=acc[:],
+                    lhsT=codes[f][:, w_cols].bitcast(E4M3_X4),
+                    lhsT_scale=scales[f][:, w_cols],
+                    rhs=g_codes[:, g_cols].bitcast(E5M2_X4),
+                    rhs_scale=g_scales[:, g_cols],
+                    start=(k == 0),
+                    stop=(k == len(terms) - 1),
+                )
+            return acc
+
+        def finish(state, part):
+            for fo in range(part * BINS_PER_PART, (part + 1) * BINS_PER_PART):
+                if fo % HALF_BINS == 0:
+                    state["planes"] = finish_pool.tile([P, HALF_BINS, N_COLS], F32, name="planes")
+                if fo == 0:
+                    state["result"] = finish_pool.tile([P, N_COLS, BINS], F32, name="result")
+                nc.scalar.copy(
+                    out=state["planes"][:, fo % HALF_BINS].rearrange("p (b q r) -> p b q r", b=BATCH, q=STEPS),
+                    in_=state["accs"][fo][:].rearrange("p (r b q) -> p b q r", r=PHASES, b=BATCH),
+                )
+                if fo % HALF_BINS == HALF_BINS - 1:
+                    half = slice(fo + 1 - HALF_BINS, fo + 1)
+                    for b in range(BATCH):
+                        cols = slice(b * FRAMES, (b + 1) * FRAMES)
+                        nc.vector.tensor_copy(
+                            out=state["result"][:, cols, half],
+                            in_=state["planes"][:, :, cols].rearrange("p f c -> p c f"),
+                        )
+                        if fo == BINS - 1:
+                            i_rows = slice(state["it"] * P, (state["it"] + 1) * P)
+                            nc.sync.dma_start(
+                                out=out[b, i_rows].rearrange("i t f -> i (t f)"),
+                                in_=state["result"][:, cols, :].rearrange("p t f -> p (t f)"),
+                            )
+
+        previous = None
         for it in range(I_TILES):
             grouped = [
                 grouped_pool.tile([P, len(kept_n(f)) * KH, P, PACK], BF16, name="grouped%d" % f, align_bytes=64)
                 for f in range(BINS)
             ]
-            for cl in range(CHUNKS_PER_TILE):
-                c = it * CHUNKS_PER_TILE + cl
-                w_src = raws[c][:].rearrange("p j (i f m n) -> p f m i j n", f=BINS, m=KH, n=KW)
-                cols = slice(cl * CHUNK, (cl + 1) * CHUNK)
-                for f in range(BINS):
-                    kept = kept_n(f)
-                    w_dst = grouped[f][:, :, cols, :].rearrange("p (m n) i j -> p m i j n", m=KH)
-                    regroup(f % 2 == 1 and f < BINS - 1, w_dst, w_src[:, f, :, :, :, kept[0] : kept[-1] + 1])
-                if c + RAW_BUFS < I_TILES * CHUNKS_PER_TILE:
-                    raws.append(load_chunk(c + RAW_BUFS))
-
             codes = []
             scales = []
-            for f in range(BINS):
-                width = len(kept_n(f)) * KH * P
-                codes.append(late.tile([P, width], U32, name="codes%d" % f, align_bytes=64))
-                scales.append(late.tile([P, width], U8, name="scales%d" % f, align_bytes=64))
-                flat = grouped[f][:].rearrange("p s i j -> p (s i j)")
-                for start, size in power_of_two_pieces(width * PACK):
-                    words = slice(start // PACK, (start + size) // PACK)
-                    nc.vector.quantize_mx(
-                        out=codes[f][:, words].bitcast(E4M3_X4),
-                        scales=scales[f][:, words],
-                        in_=flat[:, start : start + size],
-                    )
-
-            planes = late.tile([P, BINS, N_COLS], F32, name="planes")
-            result = late.tile([P, N_COLS, BINS], F32, name="result")
-            for fo in range(BINS):
-                acc = psum.tile([P, N_COLS], F32, name="acc")
-                terms = [(fo + PW - n, m, n) for n in reversed(range(KW)) for m in range(KH) if 0 <= fo + PW - n < BINS]
-                for k, (f, m, n) in enumerate(terms):
-                    w_cols = slice(slot(f, m, n) * P, (slot(f, m, n) + 1) * P)
-                    first = f * G_COLS + (PH + PH - m) * PLANE
-                    g_cols = slice(first, first + N_COLS)
-                    nc.tensor.matmul_mx(
-                        out=acc[:],
-                        lhsT=codes[f][:, w_cols].bitcast(E4M3_X4),
-                        lhsT_scale=scales[f][:, w_cols],
-                        rhs=g_codes[:, g_cols].bitcast(E5M2_X4),
-                        rhs_scale=g_scales[:, g_cols],
-                        start=(k == 0),
-                        stop=(k == len(terms) - 1),
-                    )
-                nc.scalar.copy(
-                    out=planes[:, fo].rearrange("p (b q r) -> p b q r", b=BATCH, q=STEPS),
-                    in_=acc[:].rearrange("p (r b q) -> p b q r", r=PHASES, b=BATCH),
-                )
-                if fo % HALF_BINS == HALF_BINS - 1:
-                    half = slice(fo + 1 - HALF_BINS, fo + 1)
-                    nc.vector.tensor_copy(out=result[:, :, half], in_=planes[:, half, :].rearrange("p f c -> p c f"))
-            for b in range(BATCH):
-                nc.sync.dma_start(
-                    out=out[b, it * P : (it + 1) * P].rearrange("i t f -> i (t f)"),
-                    in_=result[:, b * FRAMES : (b + 1) * FRAMES, :].rearrange("p t f -> p (t f)"),
-                )
+            for part in range(CHUNKS_PER_TILE):
+                c = it * CHUNKS_PER_TILE + part
+                for f in range(BINS):
+                    regroup_kernel(c, f, grouped)
+                    if part == CHUNKS_PER_TILE - 1:
+                        width = len(kept_n(f)) * KH * P
+                        codes.append(late.tile([P, width], U32, name="codes%d" % f, align_bytes=64))
+                        scales.append(late.tile([P, width], U8, name="scales%d" % f, align_bytes=64))
+                        quantise(E4M3_X4, codes[f], scales[f], grouped[f][:].rearrange("p s i j -> p (s i j)"))
+                load_chunk(c + RAW_BUFS)
+                if previous is not None:
+                    finish(previous, part)
+            previous = {"it": it, "accs": [multiply(fo, codes, scales) for fo in range(BINS)]}
+        for part in range(CHUNKS_PER_TILE):
+            finish(previous, part)

@@ -34,6 +34,8 @@ HALF_BINS = BINS // 2
 HALVES = 2
 BINS_PER_PART = BINS // CHUNKS_PER_TILE
 
+BIN_GROUPS = ((0,), (1, 2), (3,), (4,), (5, 6), (7,))
+
 FLOPS = 2 * COUT * N_COLS * CIN * (BINS * TAPS - 2 * KH)
 BYTES = 2 * COUT * CIN * (BINS * TAPS - 2 * KH) + 2 * BATCH * COUT * FRAMES * BINS + 4 * BATCH * CIN * FRAMES * BINS
 
@@ -42,9 +44,17 @@ def kept_n(f):
     return [n for n in range(KW) if 0 <= f + n - PW < BINS]
 
 
+def group_of(f):
+    return [g for g, group in enumerate(BIN_GROUPS) if f in group][0]
+
+
+def slots(group):
+    return sum(len(kept_n(f)) * KH for f in group)
+
+
 def slot(f, m, n):
     kept = kept_n(f)
-    return m * len(kept) + kept.index(n)
+    return slots([e for e in BIN_GROUPS[group_of(f)] if e < f]) + m * len(kept) + kept.index(n)
 
 
 def power_of_two_pieces(width):
@@ -130,12 +140,19 @@ def tile_svconv2d_pa_kernel(tc, x, kernel, bias, grad_out, out):
         late = ctx.enter_context(tc.tile_pool(name="late", bufs=1))
         finish_pool = ctx.enter_context(tc.tile_pool(name="finish", bufs=2))
 
-        def regroup_kernel(c, f, grouped):
-            kept = kept_n(f)
+        def regroup_kernel(c, g, grouped):
+            group = BIN_GROUPS[g]
+            kept = kept_n(group[0])
             cols = slice((c % CHUNKS_PER_TILE) * CHUNK, (c % CHUNKS_PER_TILE + 1) * CHUNK)
-            w_src = raws[c][:].rearrange("p j (i f m n) -> p f m i j n", f=BINS, m=KH, n=KW)
-            w_dst = grouped[f][:, :, cols, :].rearrange("p (m n) i j -> p m i j n", m=KH)
-            regroup(f % 2 == 1 and f < BINS - 1, w_dst, w_src[:, f, :, :, :, kept[0] : kept[-1] + 1])
+            w_src = raws[c][:].rearrange("p j (i a n) -> p a i j n", a=BINS * KH, n=KW)
+            w_dst = grouped[g][:, :, cols, :].rearrange("p (a n) i j -> p a i j n", n=len(kept))
+            rows = slice(group[0] * KH, (group[-1] + 1) * KH)
+            regroup(len(group) == 1, w_dst, w_src[:, rows, :, :, kept[0] : kept[-1] + 1])
+
+        def quantise_kernel(g, grouped, codes, scales):
+            codes.append(late.tile([P, slots(BIN_GROUPS[g]) * P], U32, name="codes%d" % g, align_bytes=64))
+            scales.append(late.tile([P, slots(BIN_GROUPS[g]) * P], U8, name="scales%d" % g, align_bytes=64))
+            quantise(E4M3_X4, codes[g], scales[g], grouped[g][:].rearrange("p s i j -> p (s i j)"))
 
         def multiply(fo, codes, scales):
             acc = psum.tile([P, N_COLS], F32, name="acc")
@@ -146,8 +163,8 @@ def tile_svconv2d_pa_kernel(tc, x, kernel, bias, grad_out, out):
                 g_cols = slice(first, first + N_COLS)
                 nc.tensor.matmul_mx(
                     out=acc[:],
-                    lhsT=codes[f][:, w_cols].bitcast(E4M3_X4),
-                    lhsT_scale=scales[f][:, w_cols],
+                    lhsT=codes[group_of(f)][:, w_cols].bitcast(E4M3_X4),
+                    lhsT_scale=scales[group_of(f)][:, w_cols],
                     rhs=g_codes[:, g_cols].bitcast(E5M2_X4),
                     rhs_scale=g_scales[:, g_cols],
                     start=(k == 0),
@@ -183,20 +200,19 @@ def tile_svconv2d_pa_kernel(tc, x, kernel, bias, grad_out, out):
         previous = None
         for it in range(I_TILES):
             grouped = [
-                grouped_pool.tile([P, len(kept_n(f)) * KH, P, PACK], BF16, name="grouped%d" % f, align_bytes=64)
-                for f in range(BINS)
+                grouped_pool.tile([P, slots(group), P, PACK], BF16, name="grouped%d" % g, align_bytes=64)
+                for g, group in enumerate(BIN_GROUPS)
             ]
             codes = []
             scales = []
             for part in range(CHUNKS_PER_TILE):
                 c = it * CHUNKS_PER_TILE + part
-                for f in range(BINS):
-                    regroup_kernel(c, f, grouped)
-                    if part == CHUNKS_PER_TILE - 1:
-                        width = len(kept_n(f)) * KH * P
-                        codes.append(late.tile([P, width], U32, name="codes%d" % f, align_bytes=64))
-                        scales.append(late.tile([P, width], U8, name="scales%d" % f, align_bytes=64))
-                        quantise(E4M3_X4, codes[f], scales[f], grouped[f][:].rearrange("p s i j -> p (s i j)"))
+                for g in range(len(BIN_GROUPS)):
+                    regroup_kernel(c, g, grouped)
+                    if part == CHUNKS_PER_TILE - 1 and g > 0:
+                        quantise_kernel(g - 1, grouped, codes, scales)
+                if part == CHUNKS_PER_TILE - 1:
+                    quantise_kernel(len(BIN_GROUPS) - 1, grouped, codes, scales)
                 load_chunk(c + RAW_BUFS)
                 if previous is not None:
                     finish(previous, part)

@@ -32,9 +32,8 @@ RAW_BUFS = 3
 WIDEST_QUANTISE = 4096
 HALF_BINS = BINS // 2
 HALVES = 2
-BINS_PER_PART = BINS // CHUNKS_PER_TILE
 
-BIN_GROUPS = ((0,), (1, 2), (3,), (4,), (5, 6), (7,))
+BIN_GROUPS = ((0,), (1, 2), (3,), (4,), (7,), (5, 6))
 
 FLOPS = 2 * COUT * N_COLS * CIN * (BINS * TAPS - 2 * KH)
 BYTES = 2 * COUT * CIN * (BINS * TAPS - 2 * KH) + 2 * BATCH * COUT * FRAMES * BINS + 4 * BATCH * CIN * FRAMES * BINS
@@ -172,30 +171,33 @@ def tile_svconv2d_pa_kernel(tc, x, kernel, bias, grad_out, out):
                 )
             return acc
 
-        def finish(state, part):
-            for fo in range(part * BINS_PER_PART, (part + 1) * BINS_PER_PART):
-                if fo % HALF_BINS == 0:
-                    state["planes"] = finish_pool.tile([P, HALF_BINS, N_COLS], F32, name="planes")
-                if fo == 0:
-                    state["result"] = finish_pool.tile([P, N_COLS, BINS], F32, name="result")
-                nc.scalar.copy(
-                    out=state["planes"][:, fo % HALF_BINS].rearrange("p (b q r) -> p b q r", b=BATCH, q=STEPS),
-                    in_=state["accs"][fo][:].rearrange("p (r b q) -> p b q r", r=PHASES, b=BATCH),
+        def empty_bank(done, fo):
+            if fo % HALF_BINS == 0:
+                done["planes"].append(finish_pool.tile([P, HALF_BINS, N_COLS], F32, name="planes"))
+            nc.scalar.copy(
+                out=done["planes"][fo // HALF_BINS][:, fo % HALF_BINS].rearrange("p (b q r) -> p b q r", b=BATCH, q=STEPS),
+                in_=done["accs"][fo][:].rearrange("p (r b q) -> p b q r", r=PHASES, b=BATCH),
+            )
+
+        def interleave(done, h, result):
+            for b in range(BATCH):
+                cols = slice(b * FRAMES, (b + 1) * FRAMES)
+                nc.vector.tensor_copy(
+                    out=result[:, cols, h * HALF_BINS : (h + 1) * HALF_BINS],
+                    in_=done["planes"][h][:, :, cols].rearrange("p f c -> p c f"),
                 )
-                if fo % HALF_BINS == HALF_BINS - 1:
-                    half = slice(fo + 1 - HALF_BINS, fo + 1)
-                    for b in range(BATCH):
-                        cols = slice(b * FRAMES, (b + 1) * FRAMES)
-                        nc.vector.tensor_copy(
-                            out=state["result"][:, cols, half],
-                            in_=state["planes"][:, :, cols].rearrange("p f c -> p c f"),
-                        )
-                        if fo == BINS - 1:
-                            i_rows = slice(state["it"] * P, (state["it"] + 1) * P)
-                            nc.sync.dma_start(
-                                out=out[b, i_rows].rearrange("i t f -> i (t f)"),
-                                in_=state["result"][:, cols, :].rearrange("p t f -> p (t f)"),
-                            )
+
+        def finish(done, first_bank):
+            result = finish_pool.tile([P, N_COLS, BINS], F32, name="result")
+            for h in range(HALVES):
+                for fo in range(max(first_bank, h * HALF_BINS), (h + 1) * HALF_BINS):
+                    empty_bank(done, fo)
+                interleave(done, h, result)
+            for b in range(BATCH):
+                nc.sync.dma_start(
+                    out=out[b, done["it"] * P : (done["it"] + 1) * P].rearrange("i t f -> i (t f)"),
+                    in_=result[:, b * FRAMES : (b + 1) * FRAMES, :].rearrange("p t f -> p (t f)"),
+                )
 
         previous = None
         for it in range(I_TILES):
@@ -205,17 +207,23 @@ def tile_svconv2d_pa_kernel(tc, x, kernel, bias, grad_out, out):
             ]
             codes = []
             scales = []
-            for part in range(CHUNKS_PER_TILE):
+            for part in range(CHUNKS_PER_TILE - 1):
                 c = it * CHUNKS_PER_TILE + part
                 for g in range(len(BIN_GROUPS)):
                     regroup_kernel(c, g, grouped)
-                    if part == CHUNKS_PER_TILE - 1 and g > 0:
-                        quantise_kernel(g - 1, grouped, codes, scales)
-                if part == CHUNKS_PER_TILE - 1:
-                    quantise_kernel(len(BIN_GROUPS) - 1, grouped, codes, scales)
                 load_chunk(c + RAW_BUFS)
-                if previous is not None:
-                    finish(previous, part)
-            previous = {"it": it, "accs": [multiply(fo, codes, scales) for fo in range(BINS)]}
-        for part in range(CHUNKS_PER_TILE):
-            finish(previous, part)
+            c = (it + 1) * CHUNKS_PER_TILE - 1
+            emptied = 0
+            for g in range(len(BIN_GROUPS)):
+                regroup_kernel(c, g, grouped)
+                if g > 0:
+                    quantise_kernel(g - 1, grouped, codes, scales)
+                if previous is not None and len(BIN_GROUPS[g]) == 1:
+                    empty_bank(previous, emptied)
+                    emptied += 1
+            quantise_kernel(len(BIN_GROUPS) - 1, grouped, codes, scales)
+            load_chunk(c + RAW_BUFS)
+            if previous is not None:
+                finish(previous, emptied)
+            previous = {"it": it, "planes": [], "accs": [multiply(fo, codes, scales) for fo in range(BINS)]}
+        finish(previous, 0)

@@ -28,7 +28,7 @@ CHUNK = 32
 CHUNKS_PER_TILE = P // CHUNK
 I_TILES = CIN // P
 N_CHUNKS = I_TILES * CHUNKS_PER_TILE
-RAW_BUFS = 3
+RAW_BUFS = 4
 WIDEST_QUANTISE = 4096
 HALF_BINS = BINS // 2
 HALVES = 2
@@ -188,7 +188,7 @@ def tile_svconv2d_pa_kernel(tc, x, kernel, bias, grad_out, out):
                 )
 
         def finish(done, first_bank):
-            result = finish_pool.tile([P, N_COLS, BINS], F32, name="result")
+            result = late.tile([P, N_COLS, BINS], F32, name="result")
             for h in range(HALVES):
                 for fo in range(max(first_bank, h * HALF_BINS), (h + 1) * HALF_BINS):
                     empty_bank(done, fo)

@@ -24,16 +24,16 @@ PLANE = BATCH * STEPS
 PLANES = PHASES + 2 * PH
 G_COLS = PLANES * PLANE
 
+I_TILES = CIN // P
 CHUNK = 32
 CHUNKS_PER_TILE = P // CHUNK
-I_TILES = CIN // P
-N_CHUNKS = I_TILES * CHUNKS_PER_TILE
-RAW_BUFS = 4
+LAST_PIECES = ((96, 24), (120, 8))
 WIDEST_QUANTISE = 4096
 HALF_BINS = BINS // 2
 HALVES = 2
+G_PIECES = 2
 
-BIN_GROUPS = ((0,), (1, 2), (3,), (4,), (7,), (5, 6))
+BIN_GROUPS = ((0,), (1, 2), (3, 4), (5, 6), (7,))
 
 FLOPS = 2 * COUT * N_COLS * CIN * (BINS * TAPS - 2 * KH)
 BYTES = 2 * COUT * CIN * (BINS * TAPS - 2 * KH) + 2 * BATCH * COUT * FRAMES * BINS + 4 * BATCH * CIN * FRAMES * BINS
@@ -69,15 +69,48 @@ def power_of_two_pieces(width):
     return pieces
 
 
+def make_plan():
+    A, B, C, D, E = range(5)
+    g_plan = []
+    for k in range(BATCH * G_PIECES):
+        g_plan.append(("load_g", k))
+    for c in range(CHUNKS_PER_TILE - 1):
+        g_plan.append(("load", 0, c * CHUNK, CHUNK))
+    for first, count in LAST_PIECES:
+        g_plan.append(("load", 0, first, count))
+    for k in range(BATCH * G_PIECES):
+        g_plan += [("g", "V", k, 0), ("g", "S", k, 1)]
+    for h in range(HALVES):
+        g_plan += [("g_halo", h), ("g_quantise", h)]
+    plan = []
+    for c in range(CHUNKS_PER_TILE - 1):
+        f = c * CHUNK
+        plan += [("R", "S", 0, f, CHUNK, A), ("R", "V", 0, f, CHUNK, B), ("R", "S", 0, f, CHUNK, C), ("R", "V", 0, f, CHUNK, D), ("R", "S", 0, f, CHUNK, E), ("load", 1, f, CHUNK)]
+    plan += [("R", "S", 0, 96, 24, A), ("R", "V", 0, 96, 24, B), ("R", "S", 0, 120, 8, A), ("R", "V", 0, 120, 8, B)]
+    plan += [("Q", 0, 0), ("MX", 0, 0), ("R", "S", 0, 96, 32, C), ("Q", 0, 1), ("MX", 0, 1), ("Q", 0, 2), ("MX", 0, 2)]
+    plan += [("R", "S", 0, 96, 32, E), ("Q", 0, 3), ("MX", 0, 3), ("Q", 0, 4), ("MX", 0, 4)]
+    plan += [("R", "V", 0, 96, 32, D), ("load", 1, 96, 24), ("load", 1, 120, 8)]
+    plan += [("R", "S", 1, 0, 32, A), ("EV", "S", 0, 0), ("EV", "S", 0, 1), ("R", "V", 1, 0, 32, B)]
+    plan += [("Q", 0, 5), ("MX", 0, 5), ("Q", 0, 6), ("MX", 0, 6), ("Q", 0, 7), ("MX", 0, 7)]
+    plan += [("R", "S", 1, 0, 32, C), ("R", "S", 1, 32, 32, A), ("R", "V", 1, 32, 32, B), ("R", "S", 1, 32, 32, C)]
+    plan += [("R", "V", 1, 64, 32, B), ("R", "S", 1, 64, 32, A), ("R", "V", 1, 0, 32, D), ("R", "S", 1, 64, 32, C)]
+    plan += [("R", "S", 1, 96, 24, A), ("R", "V", 1, 96, 24, B), ("EV", "S", 0, 2), ("R", "S", 1, 120, 8, A)]
+    plan += [("Q", 1, 0), ("MX", 1, 0), ("R", "V", 1, 120, 8, B), ("R", "S", 1, 96, 32, C), ("Q", 1, 1), ("MX", 1, 1), ("EV", "S", 0, 3), ("Q", 1, 2), ("MX", 1, 2)]
+    plan += [("IL", "S", 0, 0, 0), ("IL", "S", 0, 0, 1), ("EV", "S", 0, 4), ("Q", 1, 3), ("MX", 1, 3), ("EV", "S", 0, 5), ("Q", 1, 4), ("MX", 1, 4)]
+    plan += [("R", "V", 1, 32, 32, D), ("R", "V", 1, 64, 32, D), ("R", "V", 1, 96, 32, D), ("R", "S", 1, 0, 32, E), ("R", "S", 1, 32, 32, E), ("EV", "S", 0, 6), ("EV", "S", 0, 7)]
+    plan += [("IL", "S", 0, 1, 0), ("ST", 0, 0), ("IL", "S", 0, 1, 1), ("ST", 0, 1), ("R", "S", 1, 64, 32, E), ("R", "S", 1, 96, 32, E)]
+    plan += [("Q", 1, 5), ("MX", 1, 5), ("Q", 1, 6), ("MX", 1, 6), ("Q", 1, 7), ("MX", 1, 7)]
+    for fo in range(HALF_BINS):
+        plan.append(("EV", "S", 1, fo))
+    plan += [("IL", "V", 1, 0, 0), ("IL", "V", 1, 0, 1)]
+    for fo in range(HALF_BINS, BINS):
+        plan.append(("EV", "S", 1, fo))
+    plan += [("IL", "V", 1, 1, 0), ("ST", 1, 0), ("IL", "V", 1, 1, 1), ("ST", 1, 1)]
+    return g_plan, plan
+
+
 def tile_svconv2d_pa_kernel(tc, x, kernel, bias, grad_out, out):
     nc = tc.nc
-
-    def regroup(on_scalar, dst, src):
-        if on_scalar:
-            for a in range(dst.shape[1]):
-                nc.scalar.copy(out=dst[:, a], in_=src[:, a])
-        else:
-            nc.vector.tensor_copy(out=dst, in_=src)
 
     def quantise(x4, codes, scales, grouped_flat):
         for start, size in power_of_two_pieces(grouped_flat.shape[1]):
@@ -89,141 +122,175 @@ def tile_svconv2d_pa_kernel(tc, x, kernel, bias, grad_out, out):
     with ExitStack() as ctx:
         ctx.enter_context(tc.manual_schedule())
         g_pool = ctx.enter_context(tc.tile_pool(name="g_quantised", bufs=1))
-        raw_pool = ctx.enter_context(tc.tile_pool(name="raw", bufs=RAW_BUFS))
+        raw_pool = ctx.enter_context(tc.tile_pool(name="raw", bufs=CHUNKS_PER_TILE))
         grouped_pool = ctx.enter_context(tc.tile_pool(name="grouped", bufs=1))
-        psum = ctx.enter_context(tc.psum_pool(name="psum", bufs=BINS))
+        psum = ctx.enter_context(tc.psum_pool(name="psum", bufs=1))
+        pools = {}
+
+        g_codes = g_pool.tile([P, BINS * G_COLS], U32, name="g_codes", align_bytes=64)
+        g_scales = g_pool.tile([P, BINS * G_COLS], U8, name="g_scales", align_bytes=64)
 
         kernel_rows = kernel.rearrange("(p j) i f m n -> p j (i f m n)", j=PACK)
-        raws = []
+        g_tiles = {}
+        raws = {}
+        grouped = {}
+        codes = {}
+        scales = {}
+        accs = {}
+        planes = {}
+        results = {}
 
-        def load_chunk(c):
-            if c < N_CHUNKS:
-                raw = raw_pool.tile([P, PACK, CHUNK * ROW], BF16, name="raw")
-                nc.sync.dma_start(out=raw[:], in_=kernel_rows[:, :, c * CHUNK * ROW : (c + 1) * CHUNK * ROW])
-                raws.append(raw)
-
-        g_codes = g_pool.tile([P, BINS * G_COLS], U32, align_bytes=64)
-        g_scales = g_pool.tile([P, BINS * G_COLS], U8, align_bytes=64)
-        with tc.tile_pool(name="g_prepare", bufs=1) as g_prepare:
-            g_raw = g_prepare.tile([P, BATCH, PACK, FRAMES * BINS], BF16)
-            for b in range(BATCH):
-                nc.sync.dma_start(out=g_raw[:, b], in_=grad_out[b].rearrange("(p j) t f -> p j (t f)", j=PACK))
-            for c in range(RAW_BUFS):
-                load_chunk(c)
-
-            g_grouped = g_prepare.tile([P, BINS, PLANES, BATCH, STEPS, PACK], BF16, align_bytes=64)
-            nc.vector.memset(g_grouped[:, :, 0, :, 0, :], 0.0)
-            nc.vector.memset(g_grouped[:, :, PLANES - 1, :, STEPS - 1, :], 0.0)
-            for b in range(BATCH):
-                g_src = g_raw[:, b].rearrange("p j (q r f) -> p r q j f", r=PHASES, f=BINS)
-                g_dst = g_grouped[:, :, PH : PH + PHASES, b].rearrange("p f r q j -> p r q j f")
-                for h in range(HALVES):
-                    half = slice(h * HALF_BINS, (h + 1) * HALF_BINS)
-                    regroup(h == 1, g_dst[:, :, :, :, half], g_src[:, :, :, :, half])
-            for h in range(HALVES):
-                half = slice(h * HALF_BINS, (h + 1) * HALF_BINS)
-                nc.vector.tensor_copy(
-                    out=g_grouped[:, half, 0, :, 1:STEPS, :], in_=g_grouped[:, half, PHASES, :, 0 : STEPS - 1, :]
-                )
-                nc.vector.tensor_copy(
-                    out=g_grouped[:, half, PLANES - 1, :, 0 : STEPS - 1, :], in_=g_grouped[:, half, PH, :, 1:STEPS, :]
-                )
-                words = slice(h * HALF_BINS * G_COLS, (h + 1) * HALF_BINS * G_COLS)
-                quantise(
-                    E5M2_X4,
-                    g_codes[:, words],
-                    g_scales[:, words],
-                    g_grouped[:, half].rearrange("p f s b q j -> p (f s b q j)"),
-                )
-
-        late = ctx.enter_context(tc.tile_pool(name="late", bufs=1))
-        finish_pool = ctx.enter_context(tc.tile_pool(name="finish", bufs=2))
-
-        def regroup_kernel(c, g, grouped):
-            group = BIN_GROUPS[g]
-            kept = kept_n(group[0])
-            cols = slice((c % CHUNKS_PER_TILE) * CHUNK, (c % CHUNKS_PER_TILE + 1) * CHUNK)
-            w_src = raws[c][:].rearrange("p j (i a n) -> p a i j n", a=BINS * KH, n=KW)
-            w_dst = grouped[g][:, :, cols, :].rearrange("p (a n) i j -> p a i j n", n=len(kept))
-            rows = slice(group[0] * KH, (group[-1] + 1) * KH)
-            regroup(len(group) == 1, w_dst, w_src[:, rows, :, :, kept[0] : kept[-1] + 1])
-
-        def quantise_kernel(g, grouped, codes, scales):
-            codes.append(late.tile([P, slots(BIN_GROUPS[g]) * P], U32, name="codes%d" % g, align_bytes=64))
-            scales.append(late.tile([P, slots(BIN_GROUPS[g]) * P], U8, name="scales%d" % g, align_bytes=64))
-            quantise(E4M3_X4, codes[g], scales[g], grouped[g][:].rearrange("p s i j -> p (s i j)"))
-
-        def multiply(fo, codes, scales):
-            acc = psum.tile([P, N_COLS], F32, name="acc")
-            terms = [(fo + PW - n, m, n) for n in reversed(range(KW)) for m in range(KH) if 0 <= fo + PW - n < BINS]
-            for k, (f, m, n) in enumerate(terms):
-                w_cols = slice(slot(f, m, n) * P, (slot(f, m, n) + 1) * P)
-                first = f * G_COLS + (PH + PH - m) * PLANE
-                g_cols = slice(first, first + N_COLS)
-                nc.tensor.matmul_mx(
-                    out=acc[:],
-                    lhsT=codes[group_of(f)][:, w_cols].bitcast(E4M3_X4),
-                    lhsT_scale=scales[group_of(f)][:, w_cols],
-                    rhs=g_codes[:, g_cols].bitcast(E5M2_X4),
-                    rhs_scale=g_scales[:, g_cols],
-                    start=(k == 0),
-                    stop=(k == len(terms) - 1),
-                )
-            return acc
-
-        def empty_bank(done, fo):
-            if fo % HALF_BINS == 0:
-                done["planes"].append(finish_pool.tile([P, HALF_BINS, N_COLS], F32, name="planes"))
-            nc.scalar.copy(
-                out=done["planes"][fo // HALF_BINS][:, fo % HALF_BINS].rearrange("p (b q r) -> p b q r", b=BATCH, q=STEPS),
-                in_=done["accs"][fo][:].rearrange("p (r b q) -> p b q r", r=PHASES, b=BATCH),
+        def load(it, first, count):
+            c = first // CHUNK
+            if (it, c) not in raws:
+                raws[(it, c)] = raw_pool.tile([P, PACK, CHUNK * ROW], BF16, name="raw")
+            inside = first - c * CHUNK
+            nc.sync.dma_start(
+                out=raws[(it, c)][:, :, inside * ROW : (inside + count) * ROW],
+                in_=kernel_rows[:, :, (it * P + first) * ROW : (it * P + first + count) * ROW],
             )
 
-        def interleave(done, h, result):
-            for b in range(BATCH):
-                cols = slice(b * FRAMES, (b + 1) * FRAMES)
-                nc.vector.tensor_copy(
-                    out=result[:, cols, h * HALF_BINS : (h + 1) * HALF_BINS],
-                    in_=done["planes"][h][:, :, cols].rearrange("p f c -> p c f"),
-                )
+        def load_g(k):
+            b, s = divmod(k, G_PIECES)
+            piece = slice(s * FRAMES * BINS // G_PIECES, (s + 1) * FRAMES * BINS // G_PIECES)
+            nc.sync.dma_start(out=g_tiles[k][:], in_=grad_out[b].rearrange("(p j) t f -> p j (t f)", j=PACK)[:, :, piece])
 
-        def finish(done, first_bank):
-            result = late.tile([P, N_COLS, BINS], F32, name="result")
-            for h in range(HALVES):
-                for fo in range(max(first_bank, h * HALF_BINS), (h + 1) * HALF_BINS):
-                    empty_bank(done, fo)
-                interleave(done, h, result)
-            for b in range(BATCH):
-                nc.sync.dma_start(
-                    out=out[b, done["it"] * P : (done["it"] + 1) * P].rearrange("i t f -> i (t f)"),
-                    in_=result[:, b * FRAMES : (b + 1) * FRAMES, :].rearrange("p t f -> p (t f)"),
-                )
+        def g_regroup(k, h, on_vector):
+            b, s = divmod(k, G_PIECES)
+            steps = slice(s * STEPS // G_PIECES, (s + 1) * STEPS // G_PIECES)
+            half = slice(h * HALF_BINS, (h + 1) * HALF_BINS)
+            g_src = g_tiles[k][:].rearrange("p j (q r f) -> p r q j f", r=PHASES, f=BINS)[:, :, :, :, half]
+            g_dst = g_tiles["grouped"][:, :, PH : PH + PHASES, b].rearrange("p f r q j -> p r q j f")[:, :, steps, :, half]
+            if on_vector:
+                nc.vector.tensor_copy(out=g_dst, in_=g_src)
+            else:
+                nc.scalar.copy(out=g_dst, in_=g_src)
 
-        previous = None
-        for it in range(I_TILES):
-            grouped = [
-                grouped_pool.tile([P, slots(group), P, PACK], BF16, name="grouped%d" % g, align_bytes=64)
-                for g, group in enumerate(BIN_GROUPS)
-            ]
-            codes = []
-            scales = []
-            for part in range(CHUNKS_PER_TILE - 1):
-                c = it * CHUNKS_PER_TILE + part
-                for g in range(len(BIN_GROUPS)):
-                    regroup_kernel(c, g, grouped)
-                load_chunk(c + RAW_BUFS)
-            c = (it + 1) * CHUNKS_PER_TILE - 1
-            emptied = 0
-            for g in range(len(BIN_GROUPS)):
-                regroup_kernel(c, g, grouped)
-                if g > 0:
-                    quantise_kernel(g - 1, grouped, codes, scales)
-                if previous is not None and len(BIN_GROUPS[g]) == 1:
-                    empty_bank(previous, emptied)
-                    emptied += 1
-            quantise_kernel(len(BIN_GROUPS) - 1, grouped, codes, scales)
-            load_chunk(c + RAW_BUFS)
-            if previous is not None:
-                finish(previous, emptied)
-            previous = {"it": it, "planes": [], "accs": [multiply(fo, codes, scales) for fo in range(BINS)]}
-        finish(previous, 0)
+        def g_halo(h):
+            half = slice(h * HALF_BINS, (h + 1) * HALF_BINS)
+            nc.vector.tensor_copy(out=g_tiles["grouped"][:, half, 0, :, 1:STEPS, :], in_=g_tiles["grouped"][:, half, PHASES, :, 0 : STEPS - 1, :])
+            nc.vector.tensor_copy(out=g_tiles["grouped"][:, half, PLANES - 1, :, 0 : STEPS - 1, :], in_=g_tiles["grouped"][:, half, PH, :, 1:STEPS, :])
+
+        def g_quantise(h):
+            half = slice(h * HALF_BINS, (h + 1) * HALF_BINS)
+            words = slice(h * HALF_BINS * G_COLS, (h + 1) * HALF_BINS * G_COLS)
+            quantise(E5M2_X4, g_codes[:, words], g_scales[:, words], g_tiles["grouped"][:, half].rearrange("p f s b q j -> p (f s b q j)"))
+
+        def regroup(it, first, count, g, on_vector):
+            if (it, g) not in grouped:
+                grouped[(it, g)] = grouped_pool.tile([P, slots(BIN_GROUPS[g]), P, PACK], BF16, name="grouped%d" % g, align_bytes=64)
+            group = BIN_GROUPS[g]
+            kept = kept_n(group[0])
+            c = first // CHUNK
+            inside = first - c * CHUNK
+            w_src = raws[(it, c)][:, :, inside * ROW : (inside + count) * ROW].rearrange("p j (i a n) -> p a i j n", a=BINS * KH, n=KW)
+            w_dst = grouped[(it, g)][:, :, first : first + count, :].rearrange("p (a n) i j -> p a i j n", n=len(kept))
+            rows = slice(group[0] * KH, (group[-1] + 1) * KH)
+            if on_vector:
+                nc.vector.tensor_copy(out=w_dst, in_=w_src[:, rows, :, :, kept[0] : kept[-1] + 1])
+            else:
+                nc.scalar.copy(out=w_dst, in_=w_src[:, rows, :, :, kept[0] : kept[-1] + 1])
+
+        def quantise_kernel(it, f):
+            g = group_of(f)
+            if (it, g) not in codes:
+                codes[(it, g)] = pools["late"].tile([P, slots(BIN_GROUPS[g]) * P], U32, name="codes%d" % g, align_bytes=64)
+                scales[(it, g)] = pools["late"].tile([P, slots(BIN_GROUPS[g]) * P], U8, name="scales%d" % g, align_bytes=64)
+            first = slot(f, 0, kept_n(f)[0])
+            share = slots((f,))
+            words = slice(first * P, (first + share) * P)
+            quantise(
+                E4M3_X4,
+                codes[(it, g)][:, words],
+                scales[(it, g)][:, words],
+                grouped[(it, g)][:, first : first + share].rearrange("p s i j -> p (s i j)"),
+            )
+
+        def multiply(it, f):
+            g = group_of(f)
+            for n in kept_n(f):
+                fo = f + n - PW
+                if (it, fo) not in accs:
+                    accs[(it, fo)] = psum.tile([P, N_COLS], F32, name="bank%d" % fo)
+                for m in range(KH):
+                    w_cols = slice(slot(f, m, n) * P, (slot(f, m, n) + 1) * P)
+                    first = f * G_COLS + (PH + PH - m) * PLANE
+                    g_cols = slice(first, first + N_COLS)
+                    nc.tensor.matmul_mx(
+                        out=accs[(it, fo)][:],
+                        lhsT=codes[(it, g)][:, w_cols].bitcast(E4M3_X4),
+                        lhsT_scale=scales[(it, g)][:, w_cols],
+                        rhs=g_codes[:, g_cols].bitcast(E5M2_X4),
+                        rhs_scale=g_scales[:, g_cols],
+                        start=(f == max(fo - 1, 0) and m == 0),
+                        stop=(f == min(fo + 1, BINS - 1) and m == KH - 1),
+                    )
+
+        def empty_bank(it, fo, on_vector):
+            h = fo // HALF_BINS
+            if (it, h) not in planes:
+                planes[(it, h)] = pools["finish"].tile([P, HALF_BINS, N_COLS], F32, name="planes")
+            to = planes[(it, h)][:, fo % HALF_BINS].rearrange("p (b q r) -> p b q r", b=BATCH, q=STEPS)
+            frm = accs[(it, fo)][:].rearrange("p (r b q) -> p b q r", r=PHASES, b=BATCH)
+            if on_vector:
+                nc.vector.tensor_copy(out=to, in_=frm)
+            else:
+                nc.scalar.copy(out=to, in_=frm)
+
+        def interleave(it, h, b, on_vector):
+            if it not in results:
+                if it == I_TILES - 1:
+                    results[it] = raw_pool.tile([P, N_COLS, BINS], F32, name="raw")
+                else:
+                    results[it] = pools["late"].tile([P, N_COLS, BINS], F32, name="result")
+            cols = slice(b * FRAMES, (b + 1) * FRAMES)
+            half = slice(h * HALF_BINS, (h + 1) * HALF_BINS)
+            if on_vector:
+                nc.vector.tensor_copy(out=results[it][:, cols, half], in_=planes[(it, h)][:, :, cols].rearrange("p f c -> p c f"))
+            else:
+                nc.scalar.copy(out=results[it][:, cols, half], in_=planes[(it, h)][:, :, cols].rearrange("p f c -> p c f"))
+
+        def store(it, b):
+            nc.sync.dma_start(
+                out=out[b, it * P : (it + 1) * P].rearrange("i t f -> i (t f)"),
+                in_=results[it][:, b * FRAMES : (b + 1) * FRAMES, :].rearrange("p t f -> p (t f)"),
+            )
+
+        def run(step):
+            what = step[0]
+            if what == "load_g":
+                load_g(step[1])
+            elif what == "load":
+                load(step[1], step[2], step[3])
+            elif what == "g":
+                g_regroup(step[2], step[3], step[1] == "V")
+            elif what == "g_halo":
+                g_halo(step[1])
+            elif what == "g_quantise":
+                g_quantise(step[1])
+            elif what == "R":
+                regroup(step[2], step[3], step[4], step[5], step[1] == "V")
+            elif what == "Q":
+                quantise_kernel(step[1], step[2])
+            elif what == "MX":
+                multiply(step[1], step[2])
+            elif what == "EV":
+                empty_bank(step[2], step[3], step[1] == "V")
+            elif what == "IL":
+                interleave(step[2], step[3], step[4], step[1] == "V")
+            elif what == "ST":
+                store(step[1], step[2])
+
+        g_plan, plan = make_plan()
+        with tc.tile_pool(name="g_prepare", bufs=1) as g_prepare:
+            for k in range(BATCH * G_PIECES):
+                g_tiles[k] = g_prepare.tile([P, PACK, FRAMES * BINS // G_PIECES], BF16, name="g_raw%d" % k)
+            g_tiles["grouped"] = g_prepare.tile([P, BINS, PLANES, BATCH, STEPS, PACK], BF16, name="g_grouped", align_bytes=64)
+            nc.vector.memset(g_tiles["grouped"][:, :, 0, :, 0, :], 0.0)
+            nc.vector.memset(g_tiles["grouped"][:, :, PLANES - 1, :, STEPS - 1, :], 0.0)
+            for step in g_plan:
+                run(step)
+        pools["late"] = ctx.enter_context(tc.tile_pool(name="late", bufs=1))
+        pools["finish"] = ctx.enter_context(tc.tile_pool(name="finish", bufs=2))
+        for step in plan:
+            run(step)

@@ -27,11 +27,11 @@ G_COLS = PLANES * PLANE
 I_TILES = CIN // P
 CHUNK = 32
 CHUNKS_PER_TILE = P // CHUNK
-LAST_PIECES = ((96, 24), (120, 8))
+LAST_PIECES = ((96, 32),)
 WIDEST_QUANTISE = 4096
 HALF_BINS = BINS // 2
 HALVES = 2
-G_PIECES = 2
+G_PIECES = 1
 
 BIN_GROUPS = ((0,), (1, 2), (3, 4), (5, 6), (7,))
 
@@ -86,16 +86,16 @@ def make_plan():
     for c in range(CHUNKS_PER_TILE - 1):
         f = c * CHUNK
         plan += [("R", "S", 0, f, CHUNK, A), ("R", "V", 0, f, CHUNK, B), ("R", "S", 0, f, CHUNK, C), ("R", "V", 0, f, CHUNK, D), ("R", "S", 0, f, CHUNK, E), ("load", 1, f, CHUNK)]
-    plan += [("R", "S", 0, 96, 24, A), ("R", "V", 0, 96, 24, B), ("R", "S", 0, 120, 8, A), ("R", "V", 0, 120, 8, B)]
+    plan += [("R", "S", 0, 96, 32, A), ("R", "V", 0, 96, 32, B)]
     plan += [("Q", 0, 0), ("MX", 0, 0), ("R", "S", 0, 96, 32, C), ("Q", 0, 1), ("MX", 0, 1), ("Q", 0, 2), ("MX", 0, 2)]
     plan += [("R", "S", 0, 96, 32, E), ("Q", 0, 3), ("MX", 0, 3), ("Q", 0, 4), ("MX", 0, 4)]
-    plan += [("R", "V", 0, 96, 32, D), ("load", 1, 96, 24), ("load", 1, 120, 8)]
+    plan += [("R", "V", 0, 96, 32, D), ("load", 1, 96, 32)]
     plan += [("R", "S", 1, 0, 32, A), ("EV", "S", 0, 0), ("EV", "S", 0, 1), ("R", "V", 1, 0, 32, B)]
     plan += [("Q", 0, 5), ("MX", 0, 5), ("Q", 0, 6), ("MX", 0, 6), ("Q", 0, 7), ("MX", 0, 7)]
     plan += [("R", "S", 1, 0, 32, C), ("R", "S", 1, 32, 32, A), ("R", "V", 1, 32, 32, B), ("R", "S", 1, 32, 32, C)]
     plan += [("R", "V", 1, 64, 32, B), ("R", "S", 1, 64, 32, A), ("R", "V", 1, 0, 32, D), ("R", "S", 1, 64, 32, C)]
-    plan += [("R", "S", 1, 96, 24, A), ("R", "V", 1, 96, 24, B), ("EV", "S", 0, 2), ("R", "S", 1, 120, 8, A)]
-    plan += [("Q", 1, 0), ("MX", 1, 0), ("R", "V", 1, 120, 8, B), ("R", "S", 1, 96, 32, C), ("Q", 1, 1), ("MX", 1, 1), ("EV", "S", 0, 3), ("Q", 1, 2), ("MX", 1, 2)]
+    plan += [("EV", "S", 0, 2), ("R", "S", 1, 96, 32, A), ("R", "V", 1, 96, 32, B)]
+    plan += [("Q", 1, 0), ("MX", 1, 0), ("R", "S", 1, 96, 32, C), ("Q", 1, 1), ("MX", 1, 1), ("EV", "S", 0, 3), ("Q", 1, 2), ("MX", 1, 2)]
     plan += [("IL", "S", 0, 0, 0), ("IL", "S", 0, 0, 1), ("EV", "S", 0, 4), ("Q", 1, 3), ("MX", 1, 3), ("EV", "S", 0, 5), ("Q", 1, 4), ("MX", 1, 4)]
     plan += [("R", "V", 1, 32, 32, D), ("R", "V", 1, 64, 32, D), ("R", "V", 1, 96, 32, D), ("R", "S", 1, 0, 32, E), ("R", "S", 1, 32, 32, E), ("EV", "S", 0, 6), ("EV", "S", 0, 7)]
     plan += [("IL", "S", 0, 1, 0), ("ST", 0, 0), ("IL", "S", 0, 1, 1), ("ST", 0, 1), ("R", "S", 1, 64, 32, E), ("R", "S", 1, 96, 32, E)]

@@ -94,7 +94,7 @@ def make_plan():
     plan += [("Q", 0, 5), ("MX", 0, 5), ("Q", 0, 6), ("MX", 0, 6), ("Q", 0, 7), ("MX", 0, 7)]
     plan += [("R", "S", 1, 0, 32, C), ("R", "S", 1, 32, 32, A), ("R", "V", 1, 32, 32, B), ("R", "S", 1, 32, 32, C)]
     plan += [("R", "V", 1, 64, 32, B), ("R", "S", 1, 64, 32, A), ("R", "V", 1, 0, 32, D), ("R", "S", 1, 64, 32, C)]
-    plan += [("EV", "S", 0, 2), ("R", "S", 1, 96, 32, A), ("R", "V", 1, 96, 32, B)]
+    plan += [("EV", "S", 0, 2), ("WARM", 1, 3, 2, 6), ("R", "S", 1, 96, 32, A), ("R", "V", 1, 96, 32, B)]
     plan += [("Q", 1, 0), ("MX", 1, 0), ("R", "S", 1, 96, 32, C), ("Q", 1, 1), ("MX", 1, 1), ("EV", "S", 0, 3), ("Q", 1, 2), ("MX", 1, 2)]
     plan += [("IL", "S", 0, 0, 0), ("IL", "S", 0, 0, 1), ("EV", "S", 0, 4), ("Q", 1, 3), ("MX", 1, 3), ("EV", "S", 0, 5), ("Q", 1, 4), ("MX", 1, 4)]
     plan += [("R", "V", 1, 32, 32, D), ("R", "V", 1, 64, 32, D), ("R", "V", 1, 96, 32, D), ("R", "S", 1, 0, 32, E), ("R", "S", 1, 32, 32, E), ("EV", "S", 0, 6), ("EV", "S", 0, 7)]
@@ -226,6 +226,11 @@ def tile_svconv2d_pa_kernel(tc, x, kernel, bias, grad_out, out):
                         stop=(f == min(fo + 1, BINS - 1) and m == KH - 1),
                     )
 
+        def warm(it, c, bank, count):
+            idle = psum.tile([P, N_COLS], F32, name="bank%d" % bank)
+            for k in range(count):
+                nc.tensor.matmul(out=idle[:], lhsT=raws[(it, c)][:, 0, 0:P], rhs=raws[(it, c)][:, 0, 0:N_COLS], start=True, stop=True)
+
         def empty_bank(it, fo, on_vector):
             h = fo // HALF_BINS
             if (it, h) not in planes:
@@ -274,6 +279,8 @@ def tile_svconv2d_pa_kernel(tc, x, kernel, bias, grad_out, out):
                 quantise_kernel(step[1], step[2])
             elif what == "MX":
                 multiply(step[1], step[2])
+            elif what == "WARM":
+                warm(step[1], step[2], step[3], step[4])
             elif what == "EV":
                 empty_bank(step[2], step[3], step[1] == "V")
             elif what == "IL":

@@ -92,20 +92,21 @@ def make_plan():
     plan += [("R", "V", 0, 96, 32, D), ("load", 1, 96, 32)]
     plan += [("R", "S", 1, 0, 32, A), ("EV", "S", 0, 0), ("EV", "S", 0, 1), ("R", "V", 1, 0, 32, B)]
     plan += [("Q", 0, 5), ("MX", 0, 5), ("Q", 0, 6), ("MX", 0, 6), ("Q", 0, 7), ("MX", 0, 7)]
-    plan += [("R", "S", 1, 0, 32, C), ("R", "S", 1, 32, 32, A), ("R", "V", 1, 32, 32, B), ("R", "S", 1, 32, 32, C)]
-    plan += [("R", "V", 1, 64, 32, B), ("R", "S", 1, 64, 32, A), ("R", "V", 1, 0, 32, D), ("R", "S", 1, 64, 32, C)]
-    plan += [("EV", "S", 0, 2), ("WARM", 1, 3, 2, 6), ("R", "S", 1, 96, 32, A), ("R", "V", 1, 96, 32, B)]
-    plan += [("Q", 1, 0), ("MX", 1, 0), ("R", "S", 1, 96, 32, C), ("Q", 1, 1), ("MX", 1, 1), ("EV", "S", 0, 3), ("Q", 1, 2), ("MX", 1, 2)]
-    plan += [("IL", "S", 0, 0, 0), ("IL", "S", 0, 0, 1), ("EV", "S", 0, 4), ("Q", 1, 3), ("MX", 1, 3), ("EV", "S", 0, 5), ("Q", 1, 4), ("MX", 1, 4)]
-    plan += [("R", "V", 1, 32, 32, D), ("R", "V", 1, 64, 32, D), ("R", "V", 1, 96, 32, D), ("R", "S", 1, 0, 32, E), ("R", "S", 1, 32, 32, E), ("EV", "S", 0, 6), ("EV", "S", 0, 7)]
-    plan += [("IL", "S", 0, 1, 0), ("ST", 0, 0), ("IL", "S", 0, 1, 1), ("ST", 0, 1), ("R", "S", 1, 64, 32, E), ("R", "S", 1, 96, 32, E)]
-    plan += [("Q", 1, 5), ("MX", 1, 5), ("Q", 1, 6), ("MX", 1, 6), ("Q", 1, 7), ("MX", 1, 7)]
-    for fo in range(HALF_BINS):
-        plan.append(("EV", "S", 1, fo))
-    plan += [("IL", "V", 1, 0, 0), ("IL", "V", 1, 0, 1)]
-    for fo in range(HALF_BINS, BINS):
-        plan.append(("EV", "S", 1, fo))
-    plan += [("IL", "V", 1, 1, 0), ("ST", 1, 0), ("IL", "V", 1, 1, 1), ("ST", 1, 1)]
+    plan += [("R", "S", 1, 0, 32, C), ("R", "S", 1, 32, 32, A), ("R", "V", 1, 32, 32, B), ("R", "S", 1, 32, 32, C), ("R", "V", 1, 0, 32, D), ("R", "V", 1, 32, 32, D)]
+    plan += [("R", "V", 1, 64, 32, B), ("R", "S", 1, 64, 32, A), ("R", "S", 1, 64, 32, C)]
+    plan += [("EV", "S", 0, 2)]
+    plan += [("ROW", "V", 1, 96, 32, A, 0, 2), ("ROW", "V", 1, 96, 32, A, 2, 3), ("ROW", "S", 1, 96, 32, B, 0, 3), ("Q", 1, 0), ("MX", 1, 0), ("Q", 1, 1), ("MX", 1, 1)]
+    plan += [("ROW", "V", 1, 96, 32, B, 3, 5), ("ROW", "V", 1, 96, 32, B, 5, 6), ("R", "S", 1, 96, 32, C), ("EV", "S", 0, 3), ("Q", 1, 2), ("MX", 1, 2), ("Q", 1, 3), ("EV", "S", 0, 4), ("MX", 1, 3)]
+    plan += [("IL", "S", 0, 0, 0, 0, FRAMES), ("IL", "S", 0, 0, 1, 0, FRAMES), ("EV", "S", 0, 5), ("Q", 1, 4), ("MX", 1, 4)]
+    plan += [("R", "V", 1, 64, 32, D), ("R", "V", 1, 96, 32, D), ("EV", "S", 0, 6), ("EV", "S", 0, 7), ("Q", 1, 5), ("MX", 1, 5), ("Q", 1, 6), ("MX", 1, 6)]
+    plan += [("R", "S", 1, 0, 32, E), ("R", "S", 1, 32, 32, E), ("IL", "S", 0, 1, 0, 0, FRAMES), ("ST", 0, 0, 0, FRAMES), ("R", "S", 1, 64, 32, E), ("R", "S", 1, 96, 32, E)]
+    plan += [("Q", 1, 7), ("MX", 1, 7), ("IL", "V", 0, 1, 1, 0, FRAMES), ("ST", 0, 1, 0, FRAMES)]
+    plan += [("EV", "S", 1, 0), ("EV", "V", 1, 1), ("EV", "S", 1, 2), ("EV", "V", 1, 3), ("EV", "S", 1, 4)]
+    plan += [("IL", "V", 1, 0, 0, 0, FRAMES), ("IL", "V", 1, 0, 1, 0, FRAMES), ("EV", "S", 1, 5), ("EV", "S", 1, 6)]
+    half = FRAMES // 2
+    plan += [("EVB", "V", 1, 7, 0), ("EVB", "S", 1, 7, 1)]
+    plan += [("IL", "V", 1, 1, 0, 0, half), ("ST", 1, 0, 0, half), ("IL", "S", 1, 1, 1, 0, half), ("IL", "V", 1, 1, 0, half, FRAMES), ("ST", 1, 0, half, FRAMES)]
+    plan += [("ST", 1, 1, 0, half), ("IL", "V", 1, 1, 1, half, FRAMES), ("ST", 1, 1, half, FRAMES)]
     return g_plan, plan
 
 
@@ -176,7 +177,7 @@ def tile_svconv2d_pa_kernel(tc, x, kernel, bias, grad_out, out):
             words = slice(h * HALF_BINS * G_COLS, (h + 1) * HALF_BINS * G_COLS)
             quantise(E5M2_X4, g_codes[:, words], g_scales[:, words], g_tiles["grouped"][:, half].rearrange("p f s b q j -> p (f s b q j)"))
 
-        def regroup(it, first, count, g, on_vector):
+        def regroup(it, first, count, g, on_vector, first_row, end_row):
             if (it, g) not in grouped:
                 grouped[(it, g)] = grouped_pool.tile([P, slots(BIN_GROUPS[g]), P, PACK], BF16, name="grouped%d" % g, align_bytes=64)
             group = BIN_GROUPS[g]
@@ -185,7 +186,8 @@ def tile_svconv2d_pa_kernel(tc, x, kernel, bias, grad_out, out):
             inside = first - c * CHUNK
             w_src = raws[(it, c)][:, :, inside * ROW : (inside + count) * ROW].rearrange("p j (i a n) -> p a i j n", a=BINS * KH, n=KW)
             w_dst = grouped[(it, g)][:, :, first : first + count, :].rearrange("p (a n) i j -> p a i j n", n=len(kept))
-            rows = slice(group[0] * KH, (group[-1] + 1) * KH)
+            rows = slice(group[0] * KH + first_row, group[0] * KH + end_row)
+            w_dst = w_dst[:, first_row:end_row]
             if on_vector:
                 nc.vector.tensor_copy(out=w_dst, in_=w_src[:, rows, :, :, kept[0] : kept[-1] + 1])
             else:
@@ -208,57 +210,55 @@ def tile_svconv2d_pa_kernel(tc, x, kernel, bias, grad_out, out):
 
         def multiply(it, f):
             g = group_of(f)
-            for n in kept_n(f):
+            if f < BINS - 1:
+                taps = [(m, n) for m in range(KH) for n in kept_n(f)]
+            else:
+                taps = [(m, n) for n in kept_n(f) for m in range(KH)]
+            for m, n in taps:
                 fo = f + n - PW
                 if (it, fo) not in accs:
                     accs[(it, fo)] = psum.tile([P, N_COLS], F32, name="bank%d" % fo)
-                for m in range(KH):
-                    w_cols = slice(slot(f, m, n) * P, (slot(f, m, n) + 1) * P)
-                    first = f * G_COLS + (PH + PH - m) * PLANE
-                    g_cols = slice(first, first + N_COLS)
-                    nc.tensor.matmul_mx(
-                        out=accs[(it, fo)][:],
-                        lhsT=codes[(it, g)][:, w_cols].bitcast(E4M3_X4),
-                        lhsT_scale=scales[(it, g)][:, w_cols],
-                        rhs=g_codes[:, g_cols].bitcast(E5M2_X4),
-                        rhs_scale=g_scales[:, g_cols],
-                        start=(f == max(fo - 1, 0) and m == 0),
-                        stop=(f == min(fo + 1, BINS - 1) and m == KH - 1),
-                    )
+                w_cols = slice(slot(f, m, n) * P, (slot(f, m, n) + 1) * P)
+                first = f * G_COLS + (PH + PH - m) * PLANE
+                g_cols = slice(first, first + N_COLS)
+                nc.tensor.matmul_mx(
+                    out=accs[(it, fo)][:],
+                    lhsT=codes[(it, g)][:, w_cols].bitcast(E4M3_X4),
+                    lhsT_scale=scales[(it, g)][:, w_cols],
+                    rhs=g_codes[:, g_cols].bitcast(E5M2_X4),
+                    rhs_scale=g_scales[:, g_cols],
+                    start=(f == max(fo - 1, 0) and m == 0),
+                    stop=(f == min(fo + 1, BINS - 1) and m == KH - 1),
+                )
 
-        def warm(it, c, bank, count):
-            idle = psum.tile([P, N_COLS], F32, name="bank%d" % bank)
-            for k in range(count):
-                nc.tensor.matmul(out=idle[:], lhsT=raws[(it, c)][:, 0, 0:P], rhs=raws[(it, c)][:, 0, 0:N_COLS], start=True, stop=True)
-
-        def empty_bank(it, fo, on_vector):
-            h = fo // HALF_BINS
-            if (it, h) not in planes:
-                planes[(it, h)] = pools["finish"].tile([P, HALF_BINS, N_COLS], F32, name="planes")
-            to = planes[(it, h)][:, fo % HALF_BINS].rearrange("p (b q r) -> p b q r", b=BATCH, q=STEPS)
-            frm = accs[(it, fo)][:].rearrange("p (r b q) -> p b q r", r=PHASES, b=BATCH)
+        def copy(on_vector, to, frm):
             if on_vector:
                 nc.vector.tensor_copy(out=to, in_=frm)
             else:
                 nc.scalar.copy(out=to, in_=frm)
 
-        def interleave(it, h, b, on_vector):
+        def empty_bank(it, fo, on_vector, batches):
+            h = fo // HALF_BINS
+            if (it, h) not in planes:
+                planes[(it, h)] = pools["finish"].tile([P, HALF_BINS, N_COLS], F32, name="planes")
+            to = planes[(it, h)][:, fo % HALF_BINS].rearrange("p (b q r) -> p b q r", b=BATCH, q=STEPS)
+            frm = accs[(it, fo)][:].rearrange("p (r b q) -> p b q r", r=PHASES, b=BATCH)
+            copy(on_vector, to[:, batches], frm[:, batches])
+
+        def interleave(it, h, b, on_vector, first, end):
             if it not in results:
                 if it == I_TILES - 1:
                     results[it] = raw_pool.tile([P, N_COLS, BINS], F32, name="raw")
                 else:
                     results[it] = pools["late"].tile([P, N_COLS, BINS], F32, name="result")
-            cols = slice(b * FRAMES, (b + 1) * FRAMES)
+            cols = slice(b * FRAMES + first, b * FRAMES + end)
             half = slice(h * HALF_BINS, (h + 1) * HALF_BINS)
-            if on_vector:
-                nc.vector.tensor_copy(out=results[it][:, cols, half], in_=planes[(it, h)][:, :, cols].rearrange("p f c -> p c f"))
-            else:
-                nc.scalar.copy(out=results[it][:, cols, half], in_=planes[(it, h)][:, :, cols].rearrange("p f c -> p c f"))
+            copy(on_vector, results[it][:, cols, half], planes[(it, h)][:, :, cols].rearrange("p f c -> p c f"))
 
-        def store(it, b):
+        def store(it, b, first, end):
             nc.sync.dma_start(
-                out=out[b, it * P : (it + 1) * P].rearrange("i t f -> i (t f)"),
-                in_=results[it][:, b * FRAMES : (b + 1) * FRAMES, :].rearrange("p t f -> p (t f)"),
+                out=out[b, it * P : (it + 1) * P, first:end].rearrange("i t f -> i (t f)"),
+                in_=results[it][:, b * FRAMES + first : b * FRAMES + end, :].rearrange("p t f -> p (t f)"),
             )
 
         def run(step):
@@ -274,19 +274,21 @@ def tile_svconv2d_pa_kernel(tc, x, kernel, bias, grad_out, out):
             elif what == "g_quantise":
                 g_quantise(step[1])
             elif what == "R":
-                regroup(step[2], step[3], step[4], step[5], step[1] == "V")
+                regroup(step[2], step[3], step[4], step[5], step[1] == "V", 0, len(BIN_GROUPS[step[5]]) * KH)
+            elif what == "ROW":
+                regroup(step[2], step[3], step[4], step[5], step[1] == "V", step[6], step[7])
             elif what == "Q":
                 quantise_kernel(step[1], step[2])
             elif what == "MX":
                 multiply(step[1], step[2])
-            elif what == "WARM":
-                warm(step[1], step[2], step[3], step[4])
             elif what == "EV":
-                empty_bank(step[2], step[3], step[1] == "V")
+                empty_bank(step[2], step[3], step[1] == "V", slice(0, BATCH))
+            elif what == "EVB":
+                empty_bank(step[2], step[3], step[1] == "V", slice(step[4], step[4] + 1))
             elif what == "IL":
-                interleave(step[2], step[3], step[4], step[1] == "V")
+                interleave(step[2], step[3], step[4], step[1] == "V", step[5], step[6])
             elif what == "ST":
-                store(step[1], step[2])
+                store(step[1], step[2], step[3], step[4])
 
         g_plan, plan = make_plan()
         with tc.tile_pool(name="g_prepare", bufs=1) as g_prepare:

@@ -85,21 +85,24 @@ def make_plan():
     plan = []
     for c in range(CHUNKS_PER_TILE - 1):
         f = c * CHUNK
-        plan += [("R", "S", 0, f, CHUNK, A), ("R", "V", 0, f, CHUNK, B), ("R", "S", 0, f, CHUNK, C), ("R", "V", 0, f, CHUNK, D), ("R", "S", 0, f, CHUNK, E), ("load", 1, f, CHUNK)]
+        plan += [("R", "S", 0, f, CHUNK, A), ("R", "V", 0, f, CHUNK, B), ("R", "S", 0, f, CHUNK, C), ("R", "V", 0, f, CHUNK, D), ("R", "S", 0, f, CHUNK, E)]
+        if c == 1:
+            plan += [("load", 1, 0, 64)]
+        if c == 2:
+            plan += [("load", 1, 64, 32)]
     plan += [("R", "S", 0, 96, 32, A), ("R", "V", 0, 96, 32, B)]
     plan += [("Q", 0, 0), ("MX", 0, 0), ("R", "S", 0, 96, 32, C), ("Q", 0, 1), ("MX", 0, 1), ("Q", 0, 2), ("MX", 0, 2)]
     plan += [("R", "S", 0, 96, 32, E), ("Q", 0, 3), ("MX", 0, 3), ("Q", 0, 4), ("MX", 0, 4)]
-    plan += [("R", "V", 0, 96, 32, D), ("load", 1, 96, 32)]
-    plan += [("R", "S", 1, 0, 32, A), ("EV", "S", 0, 0), ("EV", "S", 0, 1), ("R", "V", 1, 0, 32, B)]
+    plan += [("R", "S", 0, 96, 32, D), ("load", 1, 96, 32), ("EV", "S", 0, 0), ("EV", "S", 0, 1)]
     plan += [("Q", 0, 5), ("MX", 0, 5), ("Q", 0, 6), ("MX", 0, 6), ("Q", 0, 7), ("MX", 0, 7)]
-    plan += [("R", "S", 1, 0, 32, C), ("R", "S", 1, 32, 32, A), ("R", "V", 1, 32, 32, B), ("R", "S", 1, 32, 32, C), ("R", "V", 1, 0, 32, D), ("R", "V", 1, 32, 32, D)]
-    plan += [("R", "V", 1, 64, 32, B), ("R", "S", 1, 64, 32, A), ("R", "S", 1, 64, 32, C)]
+    plan += [("R", "S", 1, 0, 64, A), ("R", "V", 1, 0, 64, B), ("R", "S", 1, 0, 64, C), ("R", "V", 1, 0, 64, D)]
+    plan += [("R", "V", 1, 64, 32, B), ("R", "S", 1, 64, 32, A), ("R", "V", 1, 64, 32, C)]
     plan += [("EV", "S", 0, 2)]
     plan += [("ROW", "V", 1, 96, 32, A, 0, 2), ("ROW", "V", 1, 96, 32, A, 2, 3), ("ROW", "S", 1, 96, 32, B, 0, 3), ("Q", 1, 0), ("MX", 1, 0), ("Q", 1, 1), ("MX", 1, 1)]
     plan += [("ROW", "V", 1, 96, 32, B, 3, 5), ("ROW", "V", 1, 96, 32, B, 5, 6), ("R", "S", 1, 96, 32, C), ("EV", "S", 0, 3), ("Q", 1, 2), ("MX", 1, 2), ("Q", 1, 3), ("EV", "S", 0, 4), ("MX", 1, 3)]
     plan += [("IL", "S", 0, 0, 0, 0, FRAMES), ("IL", "S", 0, 0, 1, 0, FRAMES), ("EV", "S", 0, 5), ("Q", 1, 4), ("MX", 1, 4)]
     plan += [("R", "V", 1, 64, 32, D), ("R", "V", 1, 96, 32, D), ("EV", "S", 0, 6), ("EV", "S", 0, 7), ("Q", 1, 5), ("MX", 1, 5), ("Q", 1, 6), ("MX", 1, 6)]
-    plan += [("R", "S", 1, 0, 32, E), ("R", "S", 1, 32, 32, E), ("IL", "S", 0, 1, 0, 0, FRAMES), ("ST", 0, 0, 0, FRAMES), ("R", "S", 1, 64, 32, E), ("R", "S", 1, 96, 32, E)]
+    plan += [("R", "S", 1, 0, 64, E), ("IL", "S", 0, 1, 0, 0, FRAMES), ("ST", 0, 0, 0, FRAMES), ("R", "S", 1, 64, 32, E), ("R", "S", 1, 96, 32, E)]
     plan += [("Q", 1, 7), ("MX", 1, 7), ("IL", "V", 0, 1, 1, 0, FRAMES), ("ST", 0, 1, 0, FRAMES)]
     plan += [("EV", "S", 1, 0), ("EV", "V", 1, 1), ("EV", "S", 1, 2), ("EV", "V", 1, 3), ("EV", "S", 1, 4)]
     plan += [("IL", "V", 1, 0, 0, 0, FRAMES), ("IL", "V", 1, 0, 1, 0, FRAMES), ("EV", "S", 1, 5), ("EV", "S", 1, 6)]
@@ -123,7 +126,8 @@ def tile_svconv2d_pa_kernel(tc, x, kernel, bias, grad_out, out):
     with ExitStack() as ctx:
         ctx.enter_context(tc.manual_schedule())
         g_pool = ctx.enter_context(tc.tile_pool(name="g_quantised", bufs=1))
-        raw_pool = ctx.enter_context(tc.tile_pool(name="raw", bufs=CHUNKS_PER_TILE))
+        wide_pool = ctx.enter_context(tc.tile_pool(name="wide", bufs=1))
+        raw_pool = ctx.enter_context(tc.tile_pool(name="raw", bufs=2))
         grouped_pool = ctx.enter_context(tc.tile_pool(name="grouped", bufs=1))
         psum = ctx.enter_context(tc.psum_pool(name="psum", bufs=1))
         pools = {}
@@ -142,14 +146,17 @@ def tile_svconv2d_pa_kernel(tc, x, kernel, bias, grad_out, out):
         results = {}
 
         def load(it, first, count):
-            c = first // CHUNK
-            if (it, c) not in raws:
-                raws[(it, c)] = raw_pool.tile([P, PACK, CHUNK * ROW], BF16, name="raw")
-            inside = first - c * CHUNK
-            nc.sync.dma_start(
-                out=raws[(it, c)][:, :, inside * ROW : (inside + count) * ROW],
-                in_=kernel_rows[:, :, (it * P + first) * ROW : (it * P + first + count) * ROW],
-            )
+            if count == 2 * CHUNK:
+                wide = wide_pool.tile([P, PACK, count * ROW], BF16, name="wide")
+                raws[(it, first)] = wide[:]
+            elif first < 2 * CHUNK:
+                if "wide" not in raws:
+                    raws["wide"] = wide_pool.tile([P, 2, PACK, CHUNK * ROW], BF16, name="wide")
+                raws[(it, first)] = raws["wide"][:, first // CHUNK]
+            else:
+                raw = raw_pool.tile([P, PACK, CHUNK * ROW], BF16, name="raw")
+                raws[(it, first)] = raw[:]
+            nc.sync.dma_start(out=raws[(it, first)], in_=kernel_rows[:, :, (it * P + first) * ROW : (it * P + first + count) * ROW])
 
         def load_g(k):
             b, s = divmod(k, G_PIECES)
@@ -182,9 +189,7 @@ def tile_svconv2d_pa_kernel(tc, x, kernel, bias, grad_out, out):
                 grouped[(it, g)] = grouped_pool.tile([P, slots(BIN_GROUPS[g]), P, PACK], BF16, name="grouped%d" % g, align_bytes=64)
             group = BIN_GROUPS[g]
             kept = kept_n(group[0])
-            c = first // CHUNK
-            inside = first - c * CHUNK
-            w_src = raws[(it, c)][:, :, inside * ROW : (inside + count) * ROW].rearrange("p j (i a n) -> p a i j n", a=BINS * KH, n=KW)
+            w_src = raws[(it, first)].rearrange("p j (i a n) -> p a i j n", a=BINS * KH, n=KW)
             w_dst = grouped[(it, g)][:, :, first : first + count, :].rearrange("p (a n) i j -> p a i j n", n=len(kept))
             rows = slice(group[0] * KH + first_row, group[0] * KH + end_row)
             w_dst = w_dst[:, first_row:end_row]
@@ -248,7 +253,7 @@ def tile_svconv2d_pa_kernel(tc, x, kernel, bias, grad_out, out):
         def interleave(it, h, b, on_vector, first, end):
             if it not in results:
                 if it == I_TILES - 1:
-                    results[it] = raw_pool.tile([P, N_COLS, BINS], F32, name="raw")
+                    results[it] = wide_pool.tile([P, N_COLS, BINS], F32, name="wide")
                 else:
                     results[it] = pools["late"].tile([P, N_COLS, BINS], F32, name="result")
             cols = slice(b * FRAMES + first, b * FRAMES + end)

@@ -62,7 +62,7 @@ def power_of_two_pieces(width):
     size = WIDEST_QUANTISE
     while start < width:
         if start + size <= width:
-            pieces.append((start, size))
+            pieces.append(size)
             start += size
         else:
             size //= 2
@@ -98,7 +98,7 @@ def make_plan():
     plan += [("R", "S", 1, 0, 64, A), ("R", "V", 1, 0, 64, B), ("R", "S", 1, 0, 64, C), ("R", "V", 1, 0, 64, D)]
     plan += [("R", "V", 1, 64, 32, B), ("R", "S", 1, 64, 32, A), ("R", "V", 1, 64, 32, C)]
     plan += [("EV", "S", 0, 2)]
-    plan += [("ROW", "V", 1, 96, 32, A, 0, 2), ("ROW", "V", 1, 96, 32, A, 2, 3), ("ROW", "S", 1, 96, 32, B, 0, 3), ("Q", 1, 0), ("MX", 1, 0), ("Q", 1, 1), ("MX", 1, 1)]
+    plan += [("ROW", "V", 1, 96, 32, A, 0, 2), ("ROW", "V", 1, 96, 32, A, 2, 3), ("ROW", "S", 1, 96, 32, B, 0, 3), ("Q", 1, 0, (1024, 2048)), ("MX", 1, 0), ("Q", 1, 1, (2048, 2048, 512)), ("MX", 1, 1)]
     plan += [("ROW", "V", 1, 96, 32, B, 3, 5), ("ROW", "V", 1, 96, 32, B, 5, 6), ("R", "S", 1, 96, 32, C), ("EV", "S", 0, 3), ("Q", 1, 2), ("MX", 1, 2), ("Q", 1, 3), ("EV", "S", 0, 4), ("MX", 1, 3)]
     plan += [("IL", "S", 0, 0, 0, 0, FRAMES), ("IL", "S", 0, 0, 1, 0, FRAMES), ("EV", "S", 0, 5), ("Q", 1, 4), ("MX", 1, 4)]
     plan += [("R", "V", 1, 64, 32, D), ("R", "V", 1, 96, 32, D), ("EV", "S", 0, 6), ("EV", "S", 0, 7), ("Q", 1, 5), ("MX", 1, 5), ("Q", 1, 6), ("MX", 1, 6)]
@@ -107,21 +107,24 @@ def make_plan():
     plan += [("EV", "S", 1, 0), ("EV", "V", 1, 1), ("EV", "S", 1, 2), ("EV", "V", 1, 3), ("EV", "S", 1, 4)]
     plan += [("IL", "V", 1, 0, 0, 0, FRAMES), ("IL", "V", 1, 0, 1, 0, FRAMES), ("EV", "S", 1, 5), ("EV", "S", 1, 6)]
     half = FRAMES // 2
-    plan += [("EVB", "V", 1, 7, 0), ("EVB", "S", 1, 7, 1)]
-    plan += [("IL", "V", 1, 1, 0, 0, half), ("ST", 1, 0, 0, half), ("IL", "S", 1, 1, 1, 0, half), ("IL", "V", 1, 1, 0, half, FRAMES), ("ST", 1, 0, half, FRAMES)]
-    plan += [("ST", 1, 1, 0, half), ("IL", "V", 1, 1, 1, half, FRAMES), ("ST", 1, 1, half, FRAMES)]
+    plan += [("EVB", "V", 1, 7, 0, 0, half), ("EVB", "S", 1, 7, 1, 0, FRAMES)]
+    plan += [("IL", "V", 1, 1, 0, 0, half), ("ST", 1, 0, 0, half), ("IL", "S", 1, 1, 1, 0, half)]
+    plan += [("EVB", "V", 1, 7, 0, half, FRAMES), ("IL", "V", 1, 1, 0, half, FRAMES), ("ST", 1, 0, half, FRAMES)]
+    plan += [("IL", "V", 1, 1, 1, half, FRAMES), ("ST", 1, 1, 0, FRAMES)]
     return g_plan, plan
 
 
 def tile_svconv2d_pa_kernel(tc, x, kernel, bias, grad_out, out):
     nc = tc.nc
 
-    def quantise(x4, codes, scales, grouped_flat):
-        for start, size in power_of_two_pieces(grouped_flat.shape[1]):
+    def quantise(x4, codes, scales, grouped_flat, sizes=None):
+        start = 0
+        for size in sizes or power_of_two_pieces(grouped_flat.shape[1]):
             words = slice(start // PACK, (start + size) // PACK)
             nc.vector.quantize_mx(
                 out=codes[:, words].bitcast(x4), scales=scales[:, words], in_=grouped_flat[:, start : start + size]
             )
+            start += size
 
     with ExitStack() as ctx:
         ctx.enter_context(tc.manual_schedule())
@@ -198,7 +201,7 @@ def tile_svconv2d_pa_kernel(tc, x, kernel, bias, grad_out, out):
             else:
                 nc.scalar.copy(out=w_dst, in_=w_src[:, rows, :, :, kept[0] : kept[-1] + 1])
 
-        def quantise_kernel(it, f):
+        def quantise_kernel(it, f, sizes):
             g = group_of(f)
             if (it, g) not in codes:
                 codes[(it, g)] = pools["late"].tile([P, slots(BIN_GROUPS[g]) * P], U32, name="codes%d" % g, align_bytes=64)
@@ -211,6 +214,7 @@ def tile_svconv2d_pa_kernel(tc, x, kernel, bias, grad_out, out):
                 codes[(it, g)][:, words],
                 scales[(it, g)][:, words],
                 grouped[(it, g)][:, first : first + share].rearrange("p s i j -> p (s i j)"),
+                sizes,
             )
 
         def multiply(it, f):
@@ -242,13 +246,14 @@ def tile_svconv2d_pa_kernel(tc, x, kernel, bias, grad_out, out):
             else:
                 nc.scalar.copy(out=to, in_=frm)
 
-        def empty_bank(it, fo, on_vector, batches):
+        def empty_bank(it, fo, on_vector, batches, first, end):
             h = fo // HALF_BINS
             if (it, h) not in planes:
                 planes[(it, h)] = pools["finish"].tile([P, HALF_BINS, N_COLS], F32, name="planes")
             to = planes[(it, h)][:, fo % HALF_BINS].rearrange("p (b q r) -> p b q r", b=BATCH, q=STEPS)
             frm = accs[(it, fo)][:].rearrange("p (r b q) -> p b q r", r=PHASES, b=BATCH)
-            copy(on_vector, to[:, batches], frm[:, batches])
+            steps = slice(first // PHASES, end // PHASES)
+            copy(on_vector, to[:, batches, steps], frm[:, batches, steps])
 
         def interleave(it, h, b, on_vector, first, end):
             if it not in results:
@@ -283,13 +288,13 @@ def tile_svconv2d_pa_kernel(tc, x, kernel, bias, grad_out, out):
             elif what == "ROW":
                 regroup(step[2], step[3], step[4], step[5], step[1] == "V", step[6], step[7])
             elif what == "Q":
-                quantise_kernel(step[1], step[2])
+                quantise_kernel(step[1], step[2], step[3] if len(step) > 3 else None)
             elif what == "MX":
                 multiply(step[1], step[2])
             elif what == "EV":
-                empty_bank(step[2], step[3], step[1] == "V", slice(0, BATCH))
+                empty_bank(step[2], step[3], step[1] == "V", slice(0, BATCH), 0, FRAMES)
             elif what == "EVB":
-                empty_bank(step[2], step[3], step[1] == "V", slice(step[4], step[4] + 1))
+                empty_bank(step[2], step[3], step[1] == "V", slice(step[4], step[4] + 1), step[5], step[6])
             elif what == "IL":
                 interleave(step[2], step[3], step[4], step[1] == "V", step[5], step[6])
             elif what == "ST":

@@ -95,16 +95,17 @@ def make_plan():
     plan += [("R", "S", 0, 96, 32, E), ("Q", 0, 3), ("MX", 0, 3), ("Q", 0, 4), ("MX", 0, 4)]
     plan += [("R", "S", 0, 96, 32, D), ("load", 1, 96, 32), ("EV", "S", 0, 0), ("EV", "S", 0, 1)]
     plan += [("Q", 0, 5), ("MX", 0, 5), ("Q", 0, 6), ("MX", 0, 6), ("Q", 0, 7), ("MX", 0, 7)]
-    plan += [("R", "S", 1, 0, 64, A), ("R", "V", 1, 0, 64, B), ("R", "S", 1, 0, 64, C), ("R", "V", 1, 0, 64, D)]
+    plan += [("R", "S", 1, 0, 64, A), ("R", "V", 1, 0, 64, B), ("R", "S", 1, 0, 64, C), ("R", "V", 1, 0, 48, D)]
     plan += [("R", "V", 1, 64, 32, B), ("R", "S", 1, 64, 32, A), ("R", "V", 1, 64, 32, C)]
     plan += [("EV", "S", 0, 2)]
     plan += [("ROW", "V", 1, 96, 32, A, 0, 2), ("ROW", "V", 1, 96, 32, A, 2, 3), ("ROW", "S", 1, 96, 32, B, 0, 3), ("Q", 1, 0, (1024, 2048)), ("MX", 1, 0), ("Q", 1, 1, (2048, 2048, 512)), ("MX", 1, 1)]
     plan += [("ROW", "V", 1, 96, 32, B, 3, 5), ("ROW", "V", 1, 96, 32, B, 5, 6), ("R", "S", 1, 96, 32, C), ("EV", "S", 0, 3), ("Q", 1, 2), ("MX", 1, 2), ("Q", 1, 3), ("EV", "S", 0, 4), ("MX", 1, 3)]
-    plan += [("IL", "S", 0, 0, 0, 0, FRAMES), ("IL", "S", 0, 0, 1, 0, FRAMES), ("EV", "S", 0, 5), ("Q", 1, 4), ("MX", 1, 4)]
-    plan += [("R", "V", 1, 64, 32, D), ("R", "V", 1, 96, 32, D), ("EV", "S", 0, 6), ("EV", "S", 0, 7), ("Q", 1, 5), ("MX", 1, 5), ("Q", 1, 6), ("MX", 1, 6)]
+    plan += [("R", "S", 1, 96, 32, D), ("EV", "S", 0, 5), ("Q", 1, 4), ("MX", 1, 4)]
+    plan += [("R", "V", 1, 64, 32, D), ("R", "V", 1, 48, 16, D), ("EV", "S", 0, 6), ("EV", "S", 0, 7), ("Q", 1, 5), ("MX", 1, 5), ("Q", 1, 6), ("MX", 1, 6)]
+    plan += [("IL", "V", 0, 0, 0, 0, FRAMES), ("IL", "V", 0, 0, 1, 0, FRAMES)]
     plan += [("R", "S", 1, 0, 64, E), ("IL", "S", 0, 1, 0, 0, FRAMES), ("ST", 0, 0, 0, FRAMES), ("R", "S", 1, 64, 32, E), ("R", "S", 1, 96, 32, E)]
     plan += [("Q", 1, 7), ("MX", 1, 7), ("IL", "V", 0, 1, 1, 0, FRAMES), ("ST", 0, 1, 0, FRAMES)]
-    plan += [("EV", "S", 1, 0), ("EV", "V", 1, 1), ("EV", "S", 1, 2), ("EV", "V", 1, 3), ("EV", "S", 1, 4)]
+    plan += [("EV", "S", 1, 0), ("EV", "S", 1, 1), ("EV", "S", 1, 2), ("EV", "V", 1, 3), ("EV", "S", 1, 4)]
     plan += [("IL", "V", 1, 0, 0, 0, FRAMES), ("IL", "V", 1, 0, 1, 0, FRAMES), ("EV", "S", 1, 5), ("EV", "S", 1, 6)]
     half = FRAMES // 2
     plan += [("EVB", "V", 1, 7, 0, 0, half), ("EVB", "S", 1, 7, 1, 0, FRAMES)]
@@ -141,6 +142,7 @@ def tile_svconv2d_pa_kernel(tc, x, kernel, bias, grad_out, out):
         kernel_rows = kernel.rearrange("(p j) i f m n -> p j (i f m n)", j=PACK)
         g_tiles = {}
         raws = {}
+        raw_starts = []
         grouped = {}
         codes = {}
         scales = {}
@@ -159,6 +161,7 @@ def tile_svconv2d_pa_kernel(tc, x, kernel, bias, grad_out, out):
             else:
                 raw = raw_pool.tile([P, PACK, CHUNK * ROW], BF16, name="raw")
                 raws[(it, first)] = raw[:]
+            raw_starts.append((it, first))
             nc.sync.dma_start(out=raws[(it, first)], in_=kernel_rows[:, :, (it * P + first) * ROW : (it * P + first + count) * ROW])
 
         def load_g(k):
@@ -192,7 +195,9 @@ def tile_svconv2d_pa_kernel(tc, x, kernel, bias, grad_out, out):
                 grouped[(it, g)] = grouped_pool.tile([P, slots(BIN_GROUPS[g]), P, PACK], BF16, name="grouped%d" % g, align_bytes=64)
             group = BIN_GROUPS[g]
             kept = kept_n(group[0])
-            w_src = raws[(it, first)].rearrange("p j (i a n) -> p a i j n", a=BINS * KH, n=KW)
+            base = max(k for t, k in raw_starts if t == it and k <= first)
+            inside = slice((first - base) * ROW, (first - base + count) * ROW)
+            w_src = raws[(it, base)][:, :, inside].rearrange("p j (i a n) -> p a i j n", a=BINS * KH, n=KW)
             w_dst = grouped[(it, g)][:, :, first : first + count, :].rearrange("p (a n) i j -> p a i j n", n=len(kept))
             rows = slice(group[0] * KH + first_row, group[0] * KH + end_row)
             w_dst = w_dst[:, first_row:end_row]

from contextlib import ExitStack

import concourse.mybir as mybir

BF16 = mybir.dt.bfloat16
F32 = mybir.dt.float32
U32 = mybir.dt.uint32
U8 = mybir.dt.uint8
E4M3_X4 = mybir.dt.float8_e4m3fn_x4
E5M2_X4 = mybir.dt.float8_e5m2_x4

P = 128
PACK = 4
BATCH, CIN, COUT, FRAMES, BINS, KH, KW, PH, PW = 2, 256, 512, 256, 8, 3, 3, 1, 1
assert COUT == P * PACK

TAPS = KH * KW
ROW = BINS * TAPS
N_COLS = BATCH * FRAMES

PHASES = 8
STEPS = FRAMES // PHASES
PLANE = BATCH * STEPS
PLANES = PHASES + 2 * PH
G_COLS = PLANES * PLANE

I_TILES = CIN // P
CHUNK = 32
CHUNKS_PER_TILE = P // CHUNK
LAST_PIECES = ((96, 32),)
WIDEST_QUANTISE = 4096
HALF_BINS = BINS // 2
HALVES = 2
G_PIECES = 1

BIN_GROUPS = ((0,), (1, 2), (3, 4), (5, 6), (7,))

FLOPS = 2 * COUT * N_COLS * CIN * (BINS * TAPS - 2 * KH)
BYTES = 2 * COUT * CIN * (BINS * TAPS - 2 * KH) + 2 * BATCH * COUT * FRAMES * BINS + 4 * BATCH * CIN * FRAMES * BINS


def kept_n(f):
    return [n for n in range(KW) if 0 <= f + n - PW < BINS]


def group_of(f):
    return [g for g, group in enumerate(BIN_GROUPS) if f in group][0]


def slots(group):
    return sum(len(kept_n(f)) * KH for f in group)


def slot(f, m, n):
    kept = kept_n(f)
    return slots([e for e in BIN_GROUPS[group_of(f)] if e < f]) + m * len(kept) + kept.index(n)


def power_of_two_pieces(width):
    pieces = []
    start = 0
    size = WIDEST_QUANTISE
    while start < width:
        if start + size <= width:
            pieces.append(size)
            start += size
        else:
            size //= 2
    return pieces


def make_plan():
    A, B, C, D, E = range(5)
    g_plan = []
    for k in range(BATCH * G_PIECES):
        g_plan.append(("load_g", k))
    for c in range(CHUNKS_PER_TILE - 1):
        g_plan.append(("load", 0, c * CHUNK, CHUNK))
    for first, count in LAST_PIECES:
        g_plan.append(("load", 0, first, count))
    for k in range(BATCH * G_PIECES):
        g_plan += [("g", "V", k, 0), ("g", "S", k, 1)]
    for h in range(HALVES):
        g_plan += [("g_halo", h), ("g_quantise", h)]
    plan = []
    for c in range(CHUNKS_PER_TILE - 1):
        f = c * CHUNK
        plan += [("R", "S", 0, f, CHUNK, A), ("R", "V", 0, f, CHUNK, B), ("R", "S", 0, f, CHUNK, C), ("R", "V", 0, f, CHUNK, D), ("R", "S", 0, f, CHUNK, E)]
        if c == 1:
            plan += [("load", 1, 0, 64)]
        if c == 2:
            plan += [("load", 1, 64, 32)]
    plan += [("R", "S", 0, 96, 32, A), ("R", "V", 0, 96, 32, B)]
    plan += [("Q", 0, 0), ("MX", 0, 0), ("R", "S", 0, 96, 32, C), ("Q", 0, 1), ("MX", 0, 1), ("Q", 0, 2), ("MX", 0, 2)]
    plan += [("R", "S", 0, 96, 32, E), ("Q", 0, 3), ("MX", 0, 3), ("Q", 0, 4), ("MX", 0, 4)]
    plan += [("R", "S", 0, 96, 32, D), ("load", 1, 96, 32), ("EV", "S", 0, 0), ("EV", "S", 0, 1)]
    plan += [("Q", 0, 5), ("MX", 0, 5), ("Q", 0, 6), ("MX", 0, 6), ("Q", 0, 7), ("MX", 0, 7)]
    plan += [("R", "S", 1, 0, 64, A), ("R", "V", 1, 0, 64, B), ("R", "S", 1, 0, 64, C), ("R", "V", 1, 0, 48, D)]
    plan += [("R", "V", 1, 64, 32, B), ("R", "S", 1, 64, 32, A), ("R", "V", 1, 64, 32, C)]
    plan += [("EV", "S", 0, 2)]
    plan += [("ROW", "V", 1, 96, 32, A, 0, 2), ("ROW", "V", 1, 96, 32, A, 2, 3), ("ROW", "S", 1, 96, 32, B, 0, 3), ("Q", 1, 0, (1024, 2048)), ("MX", 1, 0), ("Q", 1, 1, (2048, 2048, 512)), ("MX", 1, 1)]
    plan += [("ROW", "V", 1, 96, 32, B, 3, 5), ("ROW", "V", 1, 96, 32, B, 5, 6), ("R", "S", 1, 96, 32, C), ("EV", "S", 0, 3), ("Q", 1, 2), ("MX", 1, 2), ("Q", 1, 3), ("EV", "S", 0, 4), ("MX", 1, 3)]
    plan += [("R", "S", 1, 96, 32, D), ("EV", "S", 0, 5), ("Q", 1, 4), ("MX", 1, 4)]
    plan += [("R", "V", 1, 64, 32, D), ("R", "V", 1, 48, 16, D), ("EV", "S", 0, 6), ("EV", "S", 0, 7), ("Q", 1, 5), ("MX", 1, 5), ("Q", 1, 6), ("MX", 1, 6)]
    plan += [("IL", "V", 0, 0, 0, 0, FRAMES), ("IL", "V", 0, 0, 1, 0, FRAMES)]
    plan += [("R", "S", 1, 0, 64, E), ("IL", "S", 0, 1, 0, 0, FRAMES), ("ST", 0, 0, 0, FRAMES), ("R", "S", 1, 64, 32, E), ("R", "S", 1, 96, 32, E)]
    plan += [("Q", 1, 7), ("MX", 1, 7), ("IL", "V", 0, 1, 1, 0, FRAMES), ("ST", 0, 1, 0, FRAMES)]
    plan += [("EV", "S", 1, 0), ("EV", "S", 1, 1), ("EV", "S", 1, 2), ("EV", "V", 1, 3), ("EV", "S", 1, 4)]
    plan += [("IL", "V", 1, 0, 0, 0, FRAMES), ("IL", "V", 1, 0, 1, 0, FRAMES), ("EV", "S", 1, 5), ("EV", "S", 1, 6)]
    half = FRAMES // 2
    plan += [("EVB", "V", 1, 7, 0, 0, half), ("EVB", "S", 1, 7, 1, 0, FRAMES)]
    plan += [("IL", "V", 1, 1, 0, 0, half), ("ST", 1, 0, 0, half), ("IL", "S", 1, 1, 1, 0, half)]
    plan += [("EVB", "V", 1, 7, 0, half, FRAMES), ("IL", "V", 1, 1, 0, half, FRAMES), ("ST", 1, 0, half, FRAMES)]
    plan += [("IL", "V", 1, 1, 1, half, FRAMES), ("ST", 1, 1, 0, FRAMES)]
    return g_plan, plan


def tile_svconv2d_pa_kernel(tc, x, kernel, bias, grad_out, out):
    nc = tc.nc

    def quantise(x4, codes, scales, grouped_flat, sizes=None):
        start = 0
        for size in sizes or power_of_two_pieces(grouped_flat.shape[1]):
            words = slice(start // PACK, (start + size) // PACK)
            nc.vector.quantize_mx(
                out=codes[:, words].bitcast(x4), scales=scales[:, words], in_=grouped_flat[:, start : start + size]
            )
            start += size

    with ExitStack() as ctx:
        ctx.enter_context(tc.manual_schedule())
        g_pool = ctx.enter_context(tc.tile_pool(name="g_quantised", bufs=1))
        wide_pool = ctx.enter_context(tc.tile_pool(name="wide", bufs=1))
        raw_pool = ctx.enter_context(tc.tile_pool(name="raw", bufs=2))
        grouped_pool = ctx.enter_context(tc.tile_pool(name="grouped", bufs=1))
        psum = ctx.enter_context(tc.psum_pool(name="psum", bufs=1))
        pools = {}

        g_codes = g_pool.tile([P, BINS * G_COLS], U32, name="g_codes", align_bytes=64)
        g_scales = g_pool.tile([P, BINS * G_COLS], U8, name="g_scales", align_bytes=64)

        kernel_rows = kernel.rearrange("(p j) i f m n -> p j (i f m n)", j=PACK)
        g_tiles = {}
        raws = {}
        raw_starts = []
        grouped = {}
        codes = {}
        scales = {}
        accs = {}
        planes = {}
        results = {}

        def load(it, first, count):
            if count == 2 * CHUNK:
                wide = wide_pool.tile([P, PACK, count * ROW], BF16, name="wide")
                raws[(it, first)] = wide[:]
            elif first < 2 * CHUNK:
                if "wide" not in raws:
                    raws["wide"] = wide_pool.tile([P, 2, PACK, CHUNK * ROW], BF16, name="wide")
                raws[(it, first)] = raws["wide"][:, first // CHUNK]
            else:
                raw = raw_pool.tile([P, PACK, CHUNK * ROW], BF16, name="raw")
                raws[(it, first)] = raw[:]
            raw_starts.append((it, first))
            nc.sync.dma_start(out=raws[(it, first)], in_=kernel_rows[:, :, (it * P + first) * ROW : (it * P + first + count) * ROW])

        def load_g(k):
            b, s = divmod(k, G_PIECES)
            piece = slice(s * FRAMES * BINS // G_PIECES, (s + 1) * FRAMES * BINS // G_PIECES)
            nc.sync.dma_start(out=g_tiles[k][:], in_=grad_out[b].rearrange("(p j) t f -> p j (t f)", j=PACK)[:, :, piece])

        def g_regroup(k, h, on_vector):
            b, s = divmod(k, G_PIECES)
            steps = slice(s * STEPS // G_PIECES, (s + 1) * STEPS // G_PIECES)
            half = slice(h * HALF_BINS, (h + 1) * HALF_BINS)
            g_src = g_tiles[k][:].rearrange("p j (q r f) -> p r q j f", r=PHASES, f=BINS)[:, :, :, :, half]
            g_dst = g_tiles["grouped"][:, :, PH : PH + PHASES, b].rearrange("p f r q j -> p r q j f")[:, :, steps, :, half]
            if on_vector:
                nc.vector.tensor_copy(out=g_dst, in_=g_src)
            else:
                nc.scalar.copy(out=g_dst, in_=g_src)

        def g_halo(h):
            half = slice(h * HALF_BINS, (h + 1) * HALF_BINS)
            nc.vector.tensor_copy(out=g_tiles["grouped"][:, half, 0, :, 1:STEPS, :], in_=g_tiles["grouped"][:, half, PHASES, :, 0 : STEPS - 1, :])
            nc.vector.tensor_copy(out=g_tiles["grouped"][:, half, PLANES - 1, :, 0 : STEPS - 1, :], in_=g_tiles["grouped"][:, half, PH, :, 1:STEPS, :])

        def g_quantise(h):
            half = slice(h * HALF_BINS, (h + 1) * HALF_BINS)
            words = slice(h * HALF_BINS * G_COLS, (h + 1) * HALF_BINS * G_COLS)
            quantise(E5M2_X4, g_codes[:, words], g_scales[:, words], g_tiles["grouped"][:, half].rearrange("p f s b q j -> p (f s b q j)"))

        def regroup(it, first, count, g, on_vector, first_row, end_row):
            if (it, g) not in grouped:
                grouped[(it, g)] = grouped_pool.tile([P, slots(BIN_GROUPS[g]), P, PACK], BF16, name="grouped%d" % g, align_bytes=64)
            group = BIN_GROUPS[g]
            kept = kept_n(group[0])
            base = max(k for t, k in raw_starts if t == it and k <= first)
            inside = slice((first - base) * ROW, (first - base + count) * ROW)
            w_src = raws[(it, base)][:, :, inside].rearrange("p j (i a n) -> p a i j n", a=BINS * KH, n=KW)
            w_dst = grouped[(it, g)][:, :, first : first + count, :].rearrange("p (a n) i j -> p a i j n", n=len(kept))
            rows = slice(group[0] * KH + first_row, group[0] * KH + end_row)
            w_dst = w_dst[:, first_row:end_row]
            if on_vector:
                nc.vector.tensor_copy(out=w_dst, in_=w_src[:, rows, :, :, kept[0] : kept[-1] + 1])
            else:
                nc.scalar.copy(out=w_dst, in_=w_src[:, rows, :, :, kept[0] : kept[-1] + 1])

        def quantise_kernel(it, f, sizes):
            g = group_of(f)
            if (it, g) not in codes:
                codes[(it, g)] = pools["late"].tile([P, slots(BIN_GROUPS[g]) * P], U32, name="codes%d" % g, align_bytes=64)
                scales[(it, g)] = pools["late"].tile([P, slots(BIN_GROUPS[g]) * P], U8, name="scales%d" % g, align_bytes=64)
            first = slot(f, 0, kept_n(f)[0])
            share = slots((f,))
            words = slice(first * P, (first + share) * P)
            quantise(
                E4M3_X4,
                codes[(it, g)][:, words],
                scales[(it, g)][:, words],
                grouped[(it, g)][:, first : first + share].rearrange("p s i j -> p (s i j)"),
                sizes,
            )

        def multiply(it, f):
            g = group_of(f)
            if f < BINS - 1:
                taps = [(m, n) for m in range(KH) for n in kept_n(f)]
            else:
                taps = [(m, n) for n in kept_n(f) for m in range(KH)]
            for m, n in taps:
                fo = f + n - PW
                if (it, fo) not in accs:
                    accs[(it, fo)] = psum.tile([P, N_COLS], F32, name="bank%d" % fo)
                w_cols = slice(slot(f, m, n) * P, (slot(f, m, n) + 1) * P)
                first = f * G_COLS + (PH + PH - m) * PLANE
                g_cols = slice(first, first + N_COLS)
                nc.tensor.matmul_mx(
                    out=accs[(it, fo)][:],
                    lhsT=codes[(it, g)][:, w_cols].bitcast(E4M3_X4),
                    lhsT_scale=scales[(it, g)][:, w_cols],
                    rhs=g_codes[:, g_cols].bitcast(E5M2_X4),
                    rhs_scale=g_scales[:, g_cols],
                    start=(f == max(fo - 1, 0) and m == 0),
                    stop=(f == min(fo + 1, BINS - 1) and m == KH - 1),
                )

        def copy(on_vector, to, frm):
            if on_vector:
                nc.vector.tensor_copy(out=to, in_=frm)
            else:
                nc.scalar.copy(out=to, in_=frm)

        def empty_bank(it, fo, on_vector, batches, first, end):
            h = fo // HALF_BINS
            if (it, h) not in planes:
                planes[(it, h)] = pools["finish"].tile([P, HALF_BINS, N_COLS], F32, name="planes")
            to = planes[(it, h)][:, fo % HALF_BINS].rearrange("p (b q r) -> p b q r", b=BATCH, q=STEPS)
            frm = accs[(it, fo)][:].rearrange("p (r b q) -> p b q r", r=PHASES, b=BATCH)
            steps = slice(first // PHASES, end // PHASES)
            copy(on_vector, to[:, batches, steps], frm[:, batches, steps])

        def interleave(it, h, b, on_vector, first, end):
            if it not in results:
                if it == I_TILES - 1:
                    results[it] = wide_pool.tile([P, N_COLS, BINS], F32, name="wide")
                else:
                    results[it] = pools["late"].tile([P, N_COLS, BINS], F32, name="result")
            cols = slice(b * FRAMES + first, b * FRAMES + end)
            half = slice(h * HALF_BINS, (h + 1) * HALF_BINS)
            copy(on_vector, results[it][:, cols, half], planes[(it, h)][:, :, cols].rearrange("p f c -> p c f"))

        def store(it, b, first, end):
            nc.sync.dma_start(
                out=out[b, it * P : (it + 1) * P, first:end].rearrange("i t f -> i (t f)"),
                in_=results[it][:, b * FRAMES + first : b * FRAMES + end, :].rearrange("p t f -> p (t f)"),
            )

        def run(step):
            what = step[0]
            if what == "load_g":
                load_g(step[1])
            elif what == "load":
                load(step[1], step[2], step[3])
            elif what == "g":
                g_regroup(step[2], step[3], step[1] == "V")
            elif what == "g_halo":
                g_halo(step[1])
            elif what == "g_quantise":
                g_quantise(step[1])
            elif what == "R":
                regroup(step[2], step[3], step[4], step[5], step[1] == "V", 0, len(BIN_GROUPS[step[5]]) * KH)
            elif what == "ROW":
                regroup(step[2], step[3], step[4], step[5], step[1] == "V", step[6], step[7])
            elif what == "Q":
                quantise_kernel(step[1], step[2], step[3] if len(step) > 3 else None)
            elif what == "MX":
                multiply(step[1], step[2])
            elif what == "EV":
                empty_bank(step[2], step[3], step[1] == "V", slice(0, BATCH), 0, FRAMES)
            elif what == "EVB":
                empty_bank(step[2], step[3], step[1] == "V", slice(step[4], step[4] + 1), step[5], step[6])
            elif what == "IL":
                interleave(step[2], step[3], step[4], step[1] == "V", step[5], step[6])
            elif what == "ST":
                store(step[1], step[2], step[3], step[4])

        g_plan, plan = make_plan()
        with tc.tile_pool(name="g_prepare", bufs=1) as g_prepare:
            for k in range(BATCH * G_PIECES):
                g_tiles[k] = g_prepare.tile([P, PACK, FRAMES * BINS // G_PIECES], BF16, name="g_raw%d" % k)
            g_tiles["grouped"] = g_prepare.tile([P, BINS, PLANES, BATCH, STEPS, PACK], BF16, name="g_grouped", align_bytes=64)
            nc.vector.memset(g_tiles["grouped"][:, :, 0, :, 0, :], 0.0)
            nc.vector.memset(g_tiles["grouped"][:, :, PLANES - 1, :, STEPS - 1, :], 0.0)
            for step in g_plan:
                run(step)
        pools["late"] = ctx.enter_context(tc.tile_pool(name="late", bufs=1))
        pools["finish"] = ctx.enter_context(tc.tile_pool(name="finish", bufs=2))
        for step in plan:
            run(step)
